import numpy as np
import ml_dtypes


def mxq(x, axis, fmt="e4m3"):
    dtype, down = {"e4m3": (ml_dtypes.float8_e4m3fn, 7), "e5m2": (ml_dtypes.float8_e5m2, 14)}[fmt]
    v = np.moveaxis(np.asarray(x, np.float32).astype(ml_dtypes.bfloat16).astype(np.float64), axis, -1)
    blocks = v.reshape(v.shape[:-1] + (-1, 32))
    amax = np.abs(blocks).max(-1, keepdims=True)
    byte = np.maximum(np.where(amax > 0, np.frexp(amax)[1] - 1 + 127, 0) - down, 1)
    scale = np.exp2(byte - 127.0)
    codes = (blocks / scale).astype(np.float32).astype(dtype).astype(np.float64)
    return np.moveaxis((codes * scale).reshape(v.shape), -1, axis)


WIDE = False


def mx_kscale(k):
    if not WIDE:
        return np.ones(k)
    levels = np.array([18, -18])
    if k % 512:
        return np.exp2(np.random.permutation(np.resize(levels, k // 32))).repeat(32)
    a = np.empty((k // 512, 16))
    for p in range(k // 512):
        a[p, :8] = np.random.permutation(np.resize(levels, 8))
        for g in range(8):
            far = levels[np.abs(levels - a[p, g]) >= 10]
            a[p, g + 8] = far[np.random.randint(len(far))]
    return np.exp2(a.ravel()).repeat(32)


BF16 = ml_dtypes.bfloat16


def bf(x):
    return np.asarray(x, np.float32).astype(BF16)


def f64(x):
    return np.asarray(x).astype(np.float64)


L, B, E, H, D = 1024, 2, 1024, 8, 128
F = H * D
T = L * B


def rope_tables():
    theta = 10000.0 ** (-2.0 / D * np.arange(D // 2))
    ang = np.arange(L)[:, None] * theta[None, :]
    return np.cos(ang), np.sin(ang)


def unrope(g):
    cos, sin = rope_tables()
    g2 = g.reshape(B, H, L, D // 2, 2)
    r0 = g2[..., 0] * cos + g2[..., 1] * sin
    r1 = g2[..., 1] * cos - g2[..., 0] * sin
    return np.stack([r0, r1], axis=-1).reshape(B, H, L, D)


def setup_inputs():
    s = mx_kscale(T).reshape(L, B)
    u = mx_kscale(F)
    u = np.repeat(u[::2], 2)
    x0 = bf(np.random.standard_normal((L, B, E)))
    w0 = bf(np.random.standard_normal((F, E)) / np.sqrt(E))
    bias = bf(np.random.standard_normal(F) * 0.2)
    g = np.random.standard_normal((B, H, L, D)) * np.exp2(np.random.randint(-6, 1, (B, 1, L, 1))) * 2.0
    g = bf(g / s.T[:, None, :, None] * u.reshape(1, H, 1, D))
    y = f64(x0) @ f64(w0).T + f64(bias)
    return {"x": bf(f64(x0) * s[:, :, None]), "w": bf(f64(w0) / u[:, None]), "bias": bias,
            "y": np.asarray(y, np.float32), "grad_out": g}


def reference(x, w, bias, y, grad_out):
    dr = unrope(f64(grad_out)).transpose(2, 0, 1, 3).reshape(T, F)
    dy = dr * (f64(y).reshape(T, F) > 0.0)
    xt = f64(x).reshape(T, E)
    dx = mxq(dy, 1, "e5m2") @ mxq(f64(w), 0, "e4m3")
    dw = mxq(dy, 0, "e5m2").T @ mxq(xt, 0, "e4m3")
    return dx.reshape(L, B, E), dw

@@ -1,0 +1,402 @@
+import math
+from contextlib import ExitStack
+
+import concourse.mybir as mybir
+from concourse.masks import make_identity
+
+F32 = mybir.dt.float32
+BF16 = mybir.dt.bfloat16
+I32 = mybir.dt.int32
+U32 = mybir.dt.uint32
+U8 = mybir.dt.uint8
+E4M3X4 = mybir.dt.float8_e4m3fn_x4
+E5M2X4 = mybir.dt.float8_e5m2_x4
+ALU = mybir.AluOpType
+ACT = mybir.ActivationFunctionType
+
+L, B, E, H, D = 1024, 2, 1024, 8, 128
+F = H * D
+T = L * B
+P = 128
+PACK = 4
+G = 4
+HALF = F // 2
+HH = H // 2
+NPAIR = D // 2
+
+FLOPS = 2 * 2 * T * F * E
+BYTES = T * E * 2 + F * E * 2 + T * F * 4 + T * F * 2 + T * E * 4 + F * E * 4
+
+EXACT = 8
+PSUM_BUFS = {"gp": 2, "tr": 2, "acc": 6 - 2}
+
+
+def tile_weightlinearattention_pa_v_kernel(tc, x, w, bias, y, grad_out, out_0, out_1):
+    nc = tc.nc
+    with ExitStack() as ctx:
+        keep = ctx.enter_context(tc.tile_pool(name="keep", bufs=1))
+        stream = ctx.enter_context(tc.tile_pool(name="stream", bufs=2))
+        psum = ctx.enter_context(tc.psum_pool(name="psum", bufs=2))
+
+        x_view = x.rearrange("n c e -> (n c) e").rearrange("(g p j) e -> g p j e", p=P, j=PACK)
+        w_view = w.rearrange("(g p j) e -> g p j e", p=P, j=PACK)
+        y_view = y.rearrange("n c f -> (n c) f").rearrange("(g p j) f -> g p j f", p=P, j=PACK)
+        g_view = grad_out.rearrange("c h (g p s) d -> c g p h (s d)", p=P, s=2)
+        o0_view = out_0.rearrange("n c e -> (n c) e").rearrange("(g p j) e -> g p j e", p=P, j=PACK)
+        o1_view = out_1.rearrange("(m p) e -> m p e", p=P)
+
+        ident_bf = keep.tile([P, P], BF16, name="ident_bf", align_bytes=64)
+        ident_f = keep.tile([P, P], F32, name="ident_f", align_bytes=64)
+        npos = keep.tile([P, 8], F32, name="npos", align_bytes=64)
+        one = keep.tile([P, 1], F32, name="one", align_bytes=64)
+        warm = keep.tile([P, 1], F32, name="warm", align_bytes=64)
+        freq = keep.tile([P, NPAIR], F32, name="freq", align_bytes=64)
+        rest = keep.tile([P, EXACT], F32, name="rest", align_bytes=64)
+        turns = keep.tile([P, 8, NPAIR], F32, name="turns", align_bytes=64)
+        whole = keep.tile([P, 8, NPAIR], I32, name="whole", align_bytes=64)
+        cos_t = keep.tile([P, 8, D], F32, name="cos_t", align_bytes=64)
+        sin_t = keep.tile([P, 8, D], F32, name="sin_t", align_bytes=64)
+
+        nc.vector.memset(one[:], 1.0)
+        nc.gpsimd.iota(npos[:], pattern=[[256, 4], [1, 2]], base=0, channel_multiplier=2,
+                       allow_small_or_imprecise_dtypes=True)
+
+        y_tiles = []
+        for g in range(G):
+            yt = keep.tile([P, PACK, F], F32, name=f"y{g}", align_bytes=64)
+            y_tiles.append(yt)
+        xc = keep.tile([P, G, E], U32, name="xc", align_bytes=64)
+        xs = keep.tile([P, G, E], U8, name="xs", align_bytes=64)
+        wc = keep.tile([P, 2, E], U32, name="wc", align_bytes=64)
+        ws = keep.tile([P, 2, E], U8, name="ws", align_bytes=64)
+        tcod = keep.tile([P, 2, G, HALF], U32, name="tcod", align_bytes=64)
+        tsc = keep.tile([P, 2, G, HALF], U8, name="tsc", align_bytes=64)
+        facod = keep.tile([P, G, 512], U32, name="facod", align_bytes=64)
+        fasc = keep.tile([P, G, 512], U8, name="fasc", align_bytes=64)
+
+        g_tiles = {}
+        raws = {}
+        inters = {}
+
+        def load_g(k):
+            u, c = k // 2, k % 2
+            hf, g = u // G, u % G
+            gt = stream.tile([P, HH, 2 * D], BF16, name="gt", tag="gt", bufs=6, align_bytes=64)
+            nc.sync.dma_start(out=gt[:], in_=g_view[c, g, :, hf * HH:(hf + 1) * HH, :])
+            g_tiles[k] = gt
+
+        def load_y(g, lo, hi):
+            nc.sync.dma_start(out=y_tiles[g][:, :, lo:hi], in_=y_view[g, :, :, lo:hi])
+
+        def load_raw(which, i):
+            rt = stream.tile([P, PACK, E], BF16, name="raw", tag="raw", bufs=3, align_bytes=64)
+            nc.sync.dma_start(out=rt[:], in_=(x_view if which == "x" else w_view)[i])
+            raws[(which, i)] = rt
+
+        def frequencies():
+            nc.scalar.activation(out=warm[:], in_=one[:], func=ACT.Sin)
+            theta = [10000.0 ** (-2.0 * i / D) / (2.0 * math.pi) for i in range(NPAIR)]
+            for i in range(EXACT):
+                scale = 2.0 ** (13 - math.floor(math.log2(theta[i])))
+                hi = math.floor(theta[i] * scale) / scale
+                nc.gpsimd.memset(freq[:, i:i + 1], hi)
+                nc.scalar.activation(out=rest[:, i:i + 1], in_=one[:], func=ACT.Copy, scale=theta[i] - hi)
+            nc.vector.tensor_scalar(out=freq[:, EXACT:EXACT + 1], in0=one[:], scalar1=theta[EXACT], scalar2=None, op0=ALU.mult)
+            have = 1
+            while EXACT + have < NPAIR:
+                n = min(have, NPAIR - EXACT - have)
+                nc.vector.tensor_scalar(out=freq[:, EXACT + have:EXACT + have + n], in0=freq[:, EXACT:EXACT + n],
+                                        scalar1=10000.0 ** (-2.0 * have / D), scalar2=None, op0=ALU.mult)
+                have += n
+
+        reduced = keep.tile([P, 2, 8, NPAIR], F32, name="reduced", align_bytes=64)
+
+        def turns_rows(lo, hi):
+            n = hi - lo
+            r = slice(lo, hi)
+            uv = stream.tile([P, 2, n, NPAIR], F32, name="uv", tag="m1", bufs=2, align_bytes=64)
+            fine = stream.tile([P, n, EXACT], F32, name="fine", tag="m2", bufs=2, align_bytes=64)
+            nc.vector.tensor_tensor(out=turns[:, r], in0=npos[:, r].unsqueeze(2).to_broadcast([P, n, NPAIR]),
+                                    in1=freq[:].unsqueeze(1).to_broadcast([P, n, NPAIR]), op=ALU.mult)
+            nc.vector.tensor_tensor(out=fine[:], in0=npos[:, r].unsqueeze(2).to_broadcast([P, n, EXACT]),
+                                    in1=rest[:].unsqueeze(1).to_broadcast([P, n, EXACT]), op=ALU.mult)
+            nc.vector.tensor_copy(out=whole[:, r], in_=turns[:, r])
+            nc.vector.scalar_tensor_tensor(out=uv[:, 0], in0=whole[:, r], scalar=-1.0, in1=turns[:, r], op0=ALU.mult, op1=ALU.add)
+            nc.vector.tensor_tensor(out=uv[:, 0, :, 0:EXACT], in0=uv[:, 0, :, 0:EXACT], in1=fine[:], op=ALU.add)
+            nc.vector.tensor_scalar(out=uv[:, 1], in0=uv[:, 0], scalar1=0.25, scalar2=None, op0=ALU.add)
+            nc.vector.scalar_tensor_tensor(out=reduced[:, :, r], in0=uv[:], scalar=0.5, in1=uv[:], op0=ALU.is_gt, op1=ALU.subtract)
+
+        def sines(g):
+            tau = 2.0 * math.pi
+            r = slice(2 * g, 2 * g + 2)
+            nc.scalar.activation(out=cos_t[:, r].rearrange("p r (i e) -> p r i e", e=2),
+                                 in_=reduced[:, 1, r].unsqueeze(3).to_broadcast([P, 2, NPAIR, 2]), func=ACT.Sin, scale=-tau)
+            sin_v = sin_t[:, r].rearrange("p r (i e) -> p r i e", e=2)
+            nc.scalar.activation(out=sin_v[:, :, :, 0], in_=reduced[:, 0, r], func=ACT.Sin, scale=-tau)
+            nc.scalar.activation(out=sin_v[:, :, :, 1], in_=reduced[:, 0, r], func=ACT.Sin, scale=tau)
+
+        def piece(which, i, q):
+            if q == 0:
+                it = stream.tile([P, E, PACK], BF16, name="inter", tag="inter", bufs=2, align_bytes=64)
+                inters[(which, i)] = it
+            cols = slice(q * 256, (q + 1) * 256)
+            nc.scalar.copy(out=inters[(which, i)][:, cols, :].rearrange("p (c i) j -> p c j i", i=4),
+                           in_=raws[(which, i)][:, :, cols].rearrange("p j (c i) -> p c j i", i=4))
+
+        def quant(which, i):
+            codes, scales = (xc, xs) if which == "x" else (wc, ws)
+            nc.vector.quantize_mx(out=codes[:, i, :].bitcast(E4M3X4), scales=scales[:, i, :],
+                                  in_=inters[(which, i)][:].rearrange("p e j -> p (e j)"))
+
+        gps, ms, drs, dzs, trs, dzfs, dzis, fbs = {}, {}, {}, {}, {}, {}, {}, {}
+
+        def gather_psum(k):
+            gp = psum.tile([P, 1024], BF16, name="gp", tag="gp", bufs=PSUM_BUFS["gp"])
+            gt = g_tiles[k][:].rearrange("p h r -> p (h r)")
+            for q in range(2):
+                nc.tensor.matmul(out=gp[:, 512 * q:512 * q + 512], lhsT=ident_bf[:], rhs=gt[:, 512 * q:512 * q + 512],
+                                 start=True, stop=True)
+            gps[k] = gp
+
+        def products(k):
+            g = (k // 2) % G
+            m1 = stream.tile([P, 1024], F32, name="m1", tag="m1", bufs=2, align_bytes=64)
+            m2 = stream.tile([P, 1024], F32, name="m2", tag="m2", bufs=2, align_bytes=64)
+            gp = gps[k][:]
+            nc.vector.tensor_tensor(
+                out=m1[:].rearrange("p (s h d) -> p h s d", s=2, h=HH),
+                in0=gp.rearrange("p (h s d) -> p h s d", h=HH, s=2),
+                in1=cos_t[:, 2 * g:2 * g + 2].unsqueeze(1).to_broadcast([P, HH, 2, D]), op=ALU.mult)
+            nc.vector.tensor_tensor(
+                out=m2[:].rearrange("p (s h i e) -> p h s i e", s=2, h=HH, e=2),
+                in0=gp.rearrange("p (h s i e) -> p h s i e", h=HH, s=2, e=2)[:, :, :, :, ::-1],
+                in1=sin_t[:, 2 * g:2 * g + 2].rearrange("p s (i e) -> p s i e", e=2).unsqueeze(1).to_broadcast([P, HH, 2, NPAIR, 2]),
+                op=ALU.mult)
+            ms[k] = (m1, m2)
+
+        def add(k):
+            dr = stream.tile([P, 2, HALF], F32, name="dr", tag="dr", bufs=1, align_bytes=64)
+            m1, m2 = ms[k]
+            eng = nc.vector if k >= 15 else nc.gpsimd
+            eng.tensor_tensor(out=dr[:].rearrange("p s f -> p (s f)"), in0=m1[:], in1=m2[:], op=ALU.add)
+            drs[k] = dr
+
+        def mask(k):
+            u, c = k // 2, k % 2
+            hf, g = u // G, u % G
+            if c == 0:
+                dz = stream.tile([P, PACK, HALF], BF16, name="dz", tag="dz", bufs=2, align_bytes=64)
+                dzs[u] = dz
+            nc.vector.scalar_tensor_tensor(
+                out=dzs[u][:, c:PACK:2, :], in0=y_tiles[g][:, c:PACK:2, hf * HALF:(hf + 1) * HALF], scalar=0.0,
+                in1=drs[k][:], op0=ALU.is_gt, op1=ALU.mult)
+
+        def transposes(k):
+            u, c = k // 2, k % 2
+            words = dzs[u][:].bitcast(F32)
+            tr = psum.tile([P, 2, 2, P], F32, name="tr", tag="tr", bufs=PSUM_BUFS["tr"])
+            for s in range(2):
+                for v in range(2):
+                    nc.tensor.transpose(tr[:, s, v, :], words[:, 2 * s + c, v::2], ident_f[:])
+            trs[k] = tr
+
+        def feature_copy(k):
+            u, c = k // 2, k % 2
+            if c == 0:
+                dzf = stream.tile([P, PACK, P, PACK], BF16, name="dzf", tag="dzf", bufs=2, align_bytes=64)
+                dzfs[u] = dzf
+            nc.scalar.copy(out=dzfs[u][:].bitcast(F32)[:, c:PACK:2], in_=trs[k][:].rearrange("p s v r -> p s r v"))
+
+        def token_copy(u, eng, lo=None, hi=None):
+            if u not in dzis:
+                dzi = stream.tile([P, HALF, PACK], BF16, name="dzi", tag="dzi", bufs=1, align_bytes=64)
+                dzis[u] = dzi
+            if lo is None:
+                lo, hi = (0, 256) if eng == "S" else (256, 512)
+            dst = dzis[u][:, lo:hi, :].rearrange("p (c i) j -> p c j i", i=4)
+            srcv = dzs[u][:, :, lo:hi].rearrange("p j (c i) -> p c j i", i=4)
+            if eng == "S":
+                nc.scalar.copy(out=dst, in_=srcv)
+            else:
+                nc.vector.tensor_copy(out=dst, in_=srcv)
+
+        def quant_f(u, c=None):
+            hf, g = u // G, u % G
+            if c is not None:
+                if c == 0:
+                    fbc = stream.tile([P, 512], U32, name="fbc", tag="fbc", bufs=2, align_bytes=64)
+                    fbs_ = stream.tile([P, 512], U8, name="fbs", tag="fbs", bufs=2, align_bytes=64)
+                    fbs[u] = (fbc, fbs_)
+                for s in range(2):
+                    j = 2 * s + c
+                    cols = slice(j * P, j * P + P)
+                    nc.vector.quantize_mx(out=fbs[u][0][:, cols].bitcast(E5M2X4), scales=fbs[u][1][:, cols],
+                                          in_=dzfs[u][:, j].rearrange("p r t -> p (r t)"))
+                return
+            if hf == 0:
+                codes, scales = facod[:, g, :], fasc[:, g, :]
+            else:
+                fbc = stream.tile([P, 512], U32, name="fbc", tag="fbc", bufs=2, align_bytes=64)
+                fbs_ = stream.tile([P, 512], U8, name="fbs", tag="fbs", bufs=2, align_bytes=64)
+                fbs[u] = (fbc, fbs_)
+                codes, scales = fbc[:], fbs_[:]
+            nc.vector.quantize_mx(out=codes.bitcast(E5M2X4), scales=scales,
+                                  in_=dzfs[u][:].rearrange("p j r t -> p (j r t)"))
+
+        def quant_t(u, lo=0, hi=HALF):
+            hf, g = u // G, u % G
+            nc.vector.quantize_mx(out=tcod[:, hf, g, lo:hi].bitcast(E5M2X4), scales=tsc[:, hf, g, lo:hi],
+                                  in_=dzis[u][:, lo:hi].rearrange("p f j -> p (f j)"))
+
+        dx_stage, dw_stage, dw_acc = {}, {}, {}
+
+        def drain(dst, acc, eng):
+            if eng == "V":
+                nc.vector.tensor_copy(out=dst, in_=acc)
+            else:
+                nc.scalar.copy(out=dst, in_=acc)
+
+        def dx(u, js, engs="SS", tag="acc"):
+            g = u % G
+            ost = stream.tile([P, 2, E], F32, name="ost", tag="raw", bufs=3, align_bytes=64)
+            for jj, j in enumerate(js):
+                cols = slice(j * P, (j + 1) * P)
+                for eh in range(2):
+                    ecols = slice(eh * 512, eh * 512 + 512)
+                    acc = psum.tile([P, 512], F32, name="acc", tag=tag, bufs=PSUM_BUFS[tag])
+                    nc.tensor.matmul_mx(out=acc[:], lhsT=facod[:, g, cols].bitcast(E5M2X4), lhsT_scale=fasc[:, g, cols],
+                                        rhs=wc[:, 0, ecols].bitcast(E4M3X4), rhs_scale=ws[:, 0, ecols], start=True, stop=False)
+                    nc.tensor.matmul_mx(out=acc[:], lhsT=fbs[u][0][:, cols].bitcast(E5M2X4), lhsT_scale=fbs[u][1][:, cols],
+                                        rhs=wc[:, 1, ecols].bitcast(E4M3X4), rhs_scale=ws[:, 1, ecols], start=False, stop=True)
+                    drain(ost[:, jj, ecols], acc[:], engs[eh])
+            nc.sync.dma_start(out=o0_view[g, :, js[0]:js[1] + 1:js[1] - js[0], :], in_=ost[:])
+
+        def dw_pass(hf, m, eh, g):
+            cols = slice(m * P, (m + 1) * P)
+            ecols = slice(eh * 512, eh * 512 + 512)
+            nc.tensor.matmul_mx(out=dw_acc[(hf, m, eh)][:], lhsT=tcod[:, hf, g, cols].bitcast(E5M2X4),
+                                lhsT_scale=tsc[:, hf, g, cols], rhs=xc[:, g, ecols].bitcast(E4M3X4),
+                                rhs_scale=xs[:, g, ecols], start=(g == 0), stop=(g == G - 1))
+
+        def dw_open(hf, m, eh, tag="acc"):
+            acc = psum.tile([P, 512], F32, name="accw", tag=tag, bufs=PSUM_BUFS[tag])
+            dw_acc[(hf, m, eh)] = acc
+            for g in range(G - 1):
+                dw_pass(hf, m, eh, g)
+
+        def dw_close(hf, m, eh, eng):
+            if (hf, m // 2) not in dw_stage:
+                ostw = stream.tile([P, 2, E], F32, name="ostw", tag="inter", bufs=2, align_bytes=64)
+                dw_stage[(hf, m // 2)] = ostw
+            ostw_row = dw_stage[(hf, m // 2)][:, m % 2]
+            dw_pass(hf, m, eh, G - 1)
+            drain(ostw_row[:, eh * 512:eh * 512 + 512], dw_acc[(hf, m, eh)][:], eng)
+            if eh == 1:
+                nc.sync.dma_start(out=o1_view[hf * 4 + m], in_=ostw_row)
+
+        def dw(hf, m, eh, eng="S"):
+            dw_open(hf, m, eh)
+            dw_close(hf, m, eh, eng)
+
+        load_g(0)
+        load_g(1)
+        load_raw("x", 0)
+        load_y(0, 0, HALF)
+        load_g(2)
+        load_g(3)
+        load_raw("w", 0)
+        load_y(1, 0, F)
+        load_raw("x", 1)
+        frequencies()
+        make_identity(nc, ident_bf[:])
+        gather_psum(0)
+        turns_rows(0, 2)
+        sines(0)
+        turns_rows(2, 8)
+        make_identity(nc, ident_f[:])
+        pieces = [("x", 0, q) for q in range(4)]
+        for which, i in (("w", 0), ("x", 1), ("w", 1), ("x", 2), ("x", 3)):
+            pieces.extend([(which, i, q) for q in range(4)])
+        loads = {
+            0: [(load_g, 4), (load_raw, "w", 1), (load_g, 5)],
+            1: [(load_y, 2, 0, F)],
+            2: [(load_g, 6), (load_raw, "x", 2), (load_g, 7)],
+            3: [(load_y, 3, 0, F)],
+            4: [(load_raw, "x", 3), (load_g, 8)],
+            5: [(load_y, 0, HALF, F), (load_g, 9)],
+        }
+        piece_count = [4, 3, 3, 3, 2, 3, 2, 3, 1] + 7 * [0]
+        quants = {1: ("x", 0), 3: ("w", 0), 4: ("x", 1), 6: ("w", 1), 7: ("x", 2), 8: ("x", 3)}
+        products_at = {
+            10: [(dw, 0, 0, 0), (dw, 0, 0, 1), (dw, 0, 1, 0)],
+            11: [(dw, 0, 1, 1), (dw, 0, 2, 0), (dw, 0, 2, 1)],
+            12: [(dx, 4, (0, 1)), (dw, 0, 3, 0)],
+            13: [(dx, 4, (2, 3)), (dw, 0, 3, 1)],
+            14: [(dx, 5, (0, 1)), (dx, 5, (2, 3))],
+            15.5: [(dx, 6, (0, 1))],
+        }
+        nstep = 16
+        for k in range(nstep):
+            for item in loads.get(k, []):
+                item[0](*item[1:])
+            if k >= 6 and k + 4 < nstep:
+                load_g(k + 4)
+            if k + 1 < nstep:
+                gather_psum(k + 1)
+            products(k)
+            if k >= 2:
+                feature_copy(k - 2)
+            u = (k - 3) // 2
+            finish = k % 2 == 1 and k >= 3
+            if finish:
+                token_copy(u, "S", 0, (256, 256, 256, 256, 512, 512, 512, 512)[u])
+                if (256, 256, 256, 256, 512, 512, 512, 512)[u] < HALF:
+                    token_copy(u, "V", (256, 256, 256, 256, 512, 512, 512, 512)[u], HALF)
+            for q in range(piece_count[k]):
+                if pieces:
+                    piece(*pieces[0])
+                    pieces = pieces[1:]
+            if k in (0, 2, 4):
+                sines(k // 2 + 1)
+            if k in quants:
+                quant(*quants[k])
+            if finish:
+                quant_f(u)
+                if u < G:
+                    quant_t(u)
+            if k % 2 == 0 and k >= 12:
+                quant_t((k - 4) // 2)
+            for item in products_at.get(k, []):
+                item[0](*item[1:])
+            if k >= 1:
+                mask(k - 1)
+                transposes(k - 1)
+            for item in products_at.get(k + 0.5, []):
+                item[0](*item[1:])
+            add(k)
+        mask(15)
+        quant_t(6)
+        dw_open(1, 0, 0, "gp")
+        dw_open(1, 0, 1, "gp")
+        feature_copy(14)
+        dx(6, (2, 3), "SV")
+        transposes(15)
+        quant_f(7, 0)
+        feature_copy(15)
+        token_copy(7, "S", 0, 160)
+        token_copy(7, "V", 160, 512)
+        quant_f(7, 1)
+        quant_t(7, 0, 256)
+        quant_t(7, 256, 512)
+        dx(7, (0, 2), "SV")
+        dw_open(1, 1, 0, "tr")
+        dw_open(1, 1, 1, "tr")
+        dx(7, (1, 3), "SV")
+        dw_close(1, 0, 0, "S")
+        dw_close(1, 0, 1, "V")
+        dw_close(1, 1, 0, "S")
+        dw_close(1, 1, 1, "V")
+        dw(1, 2, 0, "S")
+        dw(1, 2, 1, "V")
+        dw(1, 3, 0, "S")
+        dw(1, 3, 1, "V")

@@ -28,7 +28,9 @@ FLOPS = 2 * 2 * T * F * E
 BYTES = T * E * 2 + F * E * 2 + T * F * 4 + T * F * 2 + T * E * 4 + F * E * 4
 
 EXACT = 8
-PSUM_BUFS = {"gp": 2, "tr": 2, "acc": 6 - 2}
+FCENG = "SSSSSSSSSSSSSSSV"
+UNITS = ((0, 0), (0, 1), (0, 2), (0, 3), (1, 0), (1, 1), (1, 2), (1, 3))
+PSUM_BUFS = {"gp": 2, "tr": 2, "acc": 4}
 
 
 def tile_weightlinearattention_pa_v_kernel(tc, x, w, bias, y, grad_out, out_0, out_1):
@@ -37,6 +39,7 @@ def tile_weightlinearattention_pa_v_kernel(tc, x, w, bias, y, grad_out, out_0, o
         keep = ctx.enter_context(tc.tile_pool(name="keep", bufs=1))
         stream = ctx.enter_context(tc.tile_pool(name="stream", bufs=2))
         psum = ctx.enter_context(tc.psum_pool(name="psum", bufs=2))
+        ctx.enter_context(tc.manual_schedule())
 
         x_view = x.rearrange("n c e -> (n c) e").rearrange("(g p j) e -> g p j e", p=P, j=PACK)
         w_view = w.rearrange("(g p j) e -> g p j e", p=P, j=PACK)
@@ -50,6 +53,7 @@ def tile_weightlinearattention_pa_v_kernel(tc, x, w, bias, y, grad_out, out_0, o
         npos = keep.tile([P, 8], F32, name="npos", align_bytes=64)
         one = keep.tile([P, 1], F32, name="one", align_bytes=64)
         warm = keep.tile([P, 1], F32, name="warm", align_bytes=64)
+        quarter = keep.tile([P, 1], F32, name="quarter", align_bytes=64)
         freq = keep.tile([P, NPAIR], F32, name="freq", align_bytes=64)
         rest = keep.tile([P, EXACT], F32, name="rest", align_bytes=64)
         turns = keep.tile([P, 8, NPAIR], F32, name="turns", align_bytes=64)
@@ -80,7 +84,7 @@ def tile_weightlinearattention_pa_v_kernel(tc, x, w, bias, y, grad_out, out_0, o
 
         def load_g(k):
             u, c = k // 2, k % 2
-            hf, g = u // G, u % G
+            hf, g = UNITS[u]
             gt = stream.tile([P, HH, 2 * D], BF16, name="gt", tag="gt", bufs=6, align_bytes=64)
             nc.sync.dma_start(out=gt[:], in_=g_view[c, g, :, hf * HH:(hf + 1) * HH, :])
             g_tiles[k] = gt
@@ -95,6 +99,7 @@ def tile_weightlinearattention_pa_v_kernel(tc, x, w, bias, y, grad_out, out_0, o
 
         def frequencies():
             nc.scalar.activation(out=warm[:], in_=one[:], func=ACT.Sin)
+            nc.vector.tensor_scalar(out=quarter[:], in0=one[:], scalar1=math.pi / 2.0, scalar2=None, op0=ALU.mult)
             theta = [10000.0 ** (-2.0 * i / D) / (2.0 * math.pi) for i in range(NPAIR)]
             for i in range(EXACT):
                 scale = 2.0 ** (13 - math.floor(math.log2(theta[i])))
@@ -114,26 +119,29 @@ def tile_weightlinearattention_pa_v_kernel(tc, x, w, bias, y, grad_out, out_0, o
         def turns_rows(lo, hi):
             n = hi - lo
             r = slice(lo, hi)
-            uv = stream.tile([P, 2, n, NPAIR], F32, name="uv", tag="m1", bufs=2, align_bytes=64)
-            fine = stream.tile([P, n, EXACT], F32, name="fine", tag="m2", bufs=2, align_bytes=64)
+            fine = stream.tile([P, 2, n, EXACT], F32, name="fine", tag="m2", bufs=2, align_bytes=64)
             nc.vector.tensor_tensor(out=turns[:, r], in0=npos[:, r].unsqueeze(2).to_broadcast([P, n, NPAIR]),
                                     in1=freq[:].unsqueeze(1).to_broadcast([P, n, NPAIR]), op=ALU.mult)
-            nc.vector.tensor_tensor(out=fine[:], in0=npos[:, r].unsqueeze(2).to_broadcast([P, n, EXACT]),
+            nc.vector.tensor_tensor(out=fine[:, 0], in0=npos[:, r].unsqueeze(2).to_broadcast([P, n, EXACT]),
                                     in1=rest[:].unsqueeze(1).to_broadcast([P, n, EXACT]), op=ALU.mult)
-            nc.vector.tensor_copy(out=whole[:, r], in_=turns[:, r])
-            nc.vector.scalar_tensor_tensor(out=uv[:, 0], in0=whole[:, r], scalar=-1.0, in1=turns[:, r], op0=ALU.mult, op1=ALU.add)
-            nc.vector.tensor_tensor(out=uv[:, 0, :, 0:EXACT], in0=uv[:, 0, :, 0:EXACT], in1=fine[:], op=ALU.add)
-            nc.vector.tensor_scalar(out=uv[:, 1], in0=uv[:, 0], scalar1=0.25, scalar2=None, op0=ALU.add)
-            nc.vector.scalar_tensor_tensor(out=reduced[:, :, r], in0=uv[:], scalar=0.5, in1=uv[:], op0=ALU.is_gt, op1=ALU.subtract)
+            nc.vector.tensor_copy(out=whole[:, r, EXACT:], in_=turns[:, r, EXACT:])
+            nc.vector.tensor_tensor(out=fine[:, 1], in0=turns[:, r, 0:EXACT], in1=fine[:, 0], op=ALU.add)
+            nc.vector.tensor_copy(out=whole[:, r, 0:EXACT], in_=fine[:, 1])
+            nc.vector.scalar_tensor_tensor(out=reduced[:, 0, r], in0=whole[:, r], scalar=-1.0, in1=turns[:, r],
+                                           op0=ALU.mult, op1=ALU.add)
+            nc.vector.tensor_tensor(out=reduced[:, 0, r, 0:EXACT], in0=reduced[:, 0, r, 0:EXACT], in1=fine[:, 0], op=ALU.add)
+            nc.vector.scalar_tensor_tensor(out=reduced[:, 1, r], in0=reduced[:, 0, r], scalar=0.25, in1=reduced[:, 0, r],
+                                           op0=ALU.is_gt, op1=ALU.subtract)
 
         def sines(g):
             tau = 2.0 * math.pi
             r = slice(2 * g, 2 * g + 2)
-            nc.scalar.activation(out=cos_t[:, r].rearrange("p r (i e) -> p r i e", e=2),
-                                 in_=reduced[:, 1, r].unsqueeze(3).to_broadcast([P, 2, NPAIR, 2]), func=ACT.Sin, scale=-tau)
             sin_v = sin_t[:, r].rearrange("p r (i e) -> p r i e", e=2)
-            nc.scalar.activation(out=sin_v[:, :, :, 0], in_=reduced[:, 0, r], func=ACT.Sin, scale=-tau)
-            nc.scalar.activation(out=sin_v[:, :, :, 1], in_=reduced[:, 0, r], func=ACT.Sin, scale=tau)
+            nc.scalar.activation(out=cos_t[:, r].rearrange("p r (i e) -> p r i e", e=2),
+                                 in_=reduced[:, 1, r].unsqueeze(3).to_broadcast([P, 2, NPAIR, 2]), func=ACT.Sin,
+                                 scale=-tau, bias=quarter[:])
+            nc.scalar.activation(out=sin_v[:, :, :, 0], in_=reduced[:, 0, r], func=ACT.Sin, scale=tau)
+            nc.scalar.activation(out=sin_v[:, :, :, 1], in_=reduced[:, 0, r], func=ACT.Sin, scale=-tau)
 
         def piece(which, i, q):
             if q == 0:
@@ -148,6 +156,12 @@ def tile_weightlinearattention_pa_v_kernel(tc, x, w, bias, y, grad_out, out_0, o
             nc.vector.quantize_mx(out=codes[:, i, :].bitcast(E4M3X4), scales=scales[:, i, :],
                                   in_=inters[(which, i)][:].rearrange("p e j -> p (e j)"))
 
+        def drain(dst, acc, eng):
+            if eng == "V":
+                nc.vector.tensor_copy(out=dst, in_=acc)
+            else:
+                nc.scalar.copy(out=dst, in_=acc)
+
         gps, ms, drs, dzs, trs, dzfs, dzis, fbs = {}, {}, {}, {}, {}, {}, {}, {}
 
         def gather_psum(k):
@@ -159,7 +173,7 @@ def tile_weightlinearattention_pa_v_kernel(tc, x, w, bias, y, grad_out, out_0, o
             gps[k] = gp
 
         def products(k):
-            g = (k // 2) % G
+            g = UNITS[k // 2][1]
             m1 = stream.tile([P, 1024], F32, name="m1", tag="m1", bufs=2, align_bytes=64)
             m2 = stream.tile([P, 1024], F32, name="m2", tag="m2", bufs=2, align_bytes=64)
             gp = gps[k][:]
@@ -177,13 +191,13 @@ def tile_weightlinearattention_pa_v_kernel(tc, x, w, bias, y, grad_out, out_0, o
         def add(k):
             dr = stream.tile([P, 2, HALF], F32, name="dr", tag="dr", bufs=1, align_bytes=64)
             m1, m2 = ms[k]
-            eng = nc.vector if k >= 15 else nc.gpsimd
+            eng = nc.vector if k >= 16 - 1 else nc.gpsimd
             eng.tensor_tensor(out=dr[:].rearrange("p s f -> p (s f)"), in0=m1[:], in1=m2[:], op=ALU.add)
             drs[k] = dr
 
         def mask(k):
             u, c = k // 2, k % 2
-            hf, g = u // G, u % G
+            hf, g = UNITS[u]
             if c == 0:
                 dz = stream.tile([P, PACK, HALF], BF16, name="dz", tag="dz", bufs=2, align_bytes=64)
                 dzs[u] = dz
@@ -205,7 +219,7 @@ def tile_weightlinearattention_pa_v_kernel(tc, x, w, bias, y, grad_out, out_0, o
             if c == 0:
                 dzf = stream.tile([P, PACK, P, PACK], BF16, name="dzf", tag="dzf", bufs=2, align_bytes=64)
                 dzfs[u] = dzf
-            nc.scalar.copy(out=dzfs[u][:].bitcast(F32)[:, c:PACK:2], in_=trs[k][:].rearrange("p s v r -> p s r v"))
+            drain(dzfs[u][:].bitcast(F32)[:, c:PACK:2], trs[k][:].rearrange("p s v r -> p s r v"), FCENG[k])
 
         def token_copy(u, eng, lo=None, hi=None):
             if u not in dzis:
@@ -221,16 +235,16 @@ def tile_weightlinearattention_pa_v_kernel(tc, x, w, bias, y, grad_out, out_0, o
                 nc.vector.tensor_copy(out=dst, in_=srcv)
 
         def quant_f(u, c=None):
-            hf, g = u // G, u % G
+            hf, g = UNITS[u]
             if c is not None:
-                if c == 0:
+                if g not in fbs:
                     fbc = stream.tile([P, 512], U32, name="fbc", tag="fbc", bufs=2, align_bytes=64)
                     fbs_ = stream.tile([P, 512], U8, name="fbs", tag="fbs", bufs=2, align_bytes=64)
-                    fbs[u] = (fbc, fbs_)
+                    fbs[g] = (fbc, fbs_)
                 for s in range(2):
                     j = 2 * s + c
                     cols = slice(j * P, j * P + P)
-                    nc.vector.quantize_mx(out=fbs[u][0][:, cols].bitcast(E5M2X4), scales=fbs[u][1][:, cols],
+                    nc.vector.quantize_mx(out=fbs[g][0][:, cols].bitcast(E5M2X4), scales=fbs[g][1][:, cols],
                                           in_=dzfs[u][:, j].rearrange("p r t -> p (r t)"))
                 return
             if hf == 0:
@@ -238,70 +252,62 @@ def tile_weightlinearattention_pa_v_kernel(tc, x, w, bias, y, grad_out, out_0, o
             else:
                 fbc = stream.tile([P, 512], U32, name="fbc", tag="fbc", bufs=2, align_bytes=64)
                 fbs_ = stream.tile([P, 512], U8, name="fbs", tag="fbs", bufs=2, align_bytes=64)
-                fbs[u] = (fbc, fbs_)
+                fbs[g] = (fbc, fbs_)
                 codes, scales = fbc[:], fbs_[:]
             nc.vector.quantize_mx(out=codes.bitcast(E5M2X4), scales=scales,
                                   in_=dzfs[u][:].rearrange("p j r t -> p (j r t)"))
 
         def quant_t(u, lo=0, hi=HALF):
-            hf, g = u // G, u % G
+            hf, g = UNITS[u]
             nc.vector.quantize_mx(out=tcod[:, hf, g, lo:hi].bitcast(E5M2X4), scales=tsc[:, hf, g, lo:hi],
                                   in_=dzis[u][:, lo:hi].rearrange("p f j -> p (f j)"))
 
-        dx_stage, dw_stage, dw_acc = {}, {}, {}
+        dx_stage, dx_acc, dw_stage, dw_acc = {}, {}, {}, {}
 
-        def drain(dst, acc, eng):
-            if eng == "V":
-                nc.vector.tensor_copy(out=dst, in_=acc)
-            else:
-                nc.scalar.copy(out=dst, in_=acc)
+        def dx(g, j, eh):
+            cols = slice(j * P, (j + 1) * P)
+            ecols = slice(eh * 512, eh * 512 + 512)
+            acc = psum.tile([P, 512], F32, name="acc", tag="acc", bufs=PSUM_BUFS["acc"])
+            dx_acc[(g, j, eh)] = acc
+            nc.tensor.matmul_mx(out=acc[:], lhsT=facod[:, g, cols].bitcast(E5M2X4), lhsT_scale=fasc[:, g, cols],
+                                rhs=wc[:, 0, ecols].bitcast(E4M3X4), rhs_scale=ws[:, 0, ecols], start=True, stop=False)
+            nc.tensor.matmul_mx(out=acc[:], lhsT=fbs[g][0][:, cols].bitcast(E5M2X4), lhsT_scale=fbs[g][1][:, cols],
+                                rhs=wc[:, 1, ecols].bitcast(E4M3X4), rhs_scale=ws[:, 1, ecols], start=False, stop=True)
 
-        def dx(u, js, engs="SS", tag="acc"):
-            g = u % G
-            ost = stream.tile([P, 2, E], F32, name="ost", tag="raw", bufs=3, align_bytes=64)
-            for jj, j in enumerate(js):
-                cols = slice(j * P, (j + 1) * P)
-                for eh in range(2):
-                    ecols = slice(eh * 512, eh * 512 + 512)
-                    acc = psum.tile([P, 512], F32, name="acc", tag=tag, bufs=PSUM_BUFS[tag])
-                    nc.tensor.matmul_mx(out=acc[:], lhsT=facod[:, g, cols].bitcast(E5M2X4), lhsT_scale=fasc[:, g, cols],
-                                        rhs=wc[:, 0, ecols].bitcast(E4M3X4), rhs_scale=ws[:, 0, ecols], start=True, stop=False)
-                    nc.tensor.matmul_mx(out=acc[:], lhsT=fbs[u][0][:, cols].bitcast(E5M2X4), lhsT_scale=fbs[u][1][:, cols],
-                                        rhs=wc[:, 1, ecols].bitcast(E4M3X4), rhs_scale=ws[:, 1, ecols], start=False, stop=True)
-                    drain(ost[:, jj, ecols], acc[:], engs[eh])
-            nc.sync.dma_start(out=o0_view[g, :, js[0]:js[1] + 1:js[1] - js[0], :], in_=ost[:])
+        def dx_drain(g, js, j, eh, eng):
+            if (g, js) not in dx_stage:
+                ost = stream.tile([P, 2, E], F32, name="ost", tag="raw", bufs=3, align_bytes=64)
+                dx_stage[(g, js)] = ost
+            drain(dx_stage[(g, js)][:, js.index(j), eh * 512:eh * 512 + 512], dx_acc[(g, j, eh)][:], eng)
 
-        def dw_pass(hf, m, eh, g):
+        def dx_store(g, js):
+            nc.sync.dma_start(out=o0_view[g, :, js[0]:js[1] + 1:js[1] - js[0], :], in_=dx_stage[(g, js)][:])
+
+        def dw(hf, b, g, pool):
+            m, eh = b // 2, b % 2
             cols = slice(m * P, (m + 1) * P)
             ecols = slice(eh * 512, eh * 512 + 512)
-            nc.tensor.matmul_mx(out=dw_acc[(hf, m, eh)][:], lhsT=tcod[:, hf, g, cols].bitcast(E5M2X4),
+            if g == 0:
+                accw = psum.tile([P, 512], F32, name="accw", tag=pool, bufs=PSUM_BUFS[pool])
+                dw_acc[(hf, b)] = accw
+            nc.tensor.matmul_mx(out=dw_acc[(hf, b)][:], lhsT=tcod[:, hf, g, cols].bitcast(E5M2X4),
                                 lhsT_scale=tsc[:, hf, g, cols], rhs=xc[:, g, ecols].bitcast(E4M3X4),
                                 rhs_scale=xs[:, g, ecols], start=(g == 0), stop=(g == G - 1))
 
-        def dw_open(hf, m, eh, tag="acc"):
-            acc = psum.tile([P, 512], F32, name="accw", tag=tag, bufs=PSUM_BUFS[tag])
-            dw_acc[(hf, m, eh)] = acc
-            for g in range(G - 1):
-                dw_pass(hf, m, eh, g)
-
-        def dw_close(hf, m, eh, eng):
+        def dw_drain(hf, b, eng):
+            m, eh = b // 2, b % 2
             if (hf, m // 2) not in dw_stage:
                 ostw = stream.tile([P, 2, E], F32, name="ostw", tag="inter", bufs=2, align_bytes=64)
                 dw_stage[(hf, m // 2)] = ostw
-            ostw_row = dw_stage[(hf, m // 2)][:, m % 2]
-            dw_pass(hf, m, eh, G - 1)
-            drain(ostw_row[:, eh * 512:eh * 512 + 512], dw_acc[(hf, m, eh)][:], eng)
-            if eh == 1:
-                nc.sync.dma_start(out=o1_view[hf * 4 + m], in_=ostw_row)
+            drain(dw_stage[(hf, m // 2)][:, m % 2, eh * 512:eh * 512 + 512], dw_acc[(hf, b)][:], eng)
 
-        def dw(hf, m, eh, eng="S"):
-            dw_open(hf, m, eh)
-            dw_close(hf, m, eh, eng)
+        def dw_store(hf, m):
+            nc.sync.dma_start(out=o1_view[hf * 4 + m], in_=dw_stage[(hf, m // 2)][:, m % 2])
 
         load_g(0)
         load_g(1)
         load_raw("x", 0)
-        load_y(0, 0, HALF)
+        load_y(0, 0, 512)
         load_g(2)
         load_g(3)
         load_raw("w", 0)
@@ -309,94 +315,342 @@ def tile_weightlinearattention_pa_v_kernel(tc, x, w, bias, y, grad_out, out_0, o
         load_raw("x", 1)
         frequencies()
         make_identity(nc, ident_bf[:])
-        gather_psum(0)
+        make_identity(nc, ident_f[:])
         turns_rows(0, 2)
         sines(0)
+        piece("x", 0, 0)
         turns_rows(2, 8)
-        make_identity(nc, ident_f[:])
-        pieces = [("x", 0, q) for q in range(4)]
-        for which, i in (("w", 0), ("x", 1), ("w", 1), ("x", 2), ("x", 3)):
-            pieces.extend([(which, i, q) for q in range(4)])
-        loads = {
-            0: [(load_g, 4), (load_raw, "w", 1), (load_g, 5)],
-            1: [(load_y, 2, 0, F)],
-            2: [(load_g, 6), (load_raw, "x", 2), (load_g, 7)],
-            3: [(load_y, 3, 0, F)],
-            4: [(load_raw, "x", 3), (load_g, 8)],
-            5: [(load_y, 0, HALF, F), (load_g, 9)],
-        }
-        piece_count = [4, 3, 3, 3, 2, 3, 2, 3, 1] + 7 * [0]
-        quants = {1: ("x", 0), 3: ("w", 0), 4: ("x", 1), 6: ("w", 1), 7: ("x", 2), 8: ("x", 3)}
-        products_at = {
-            10: [(dw, 0, 0, 0), (dw, 0, 0, 1), (dw, 0, 1, 0)],
-            11: [(dw, 0, 1, 1), (dw, 0, 2, 0), (dw, 0, 2, 1)],
-            12: [(dx, 4, (0, 1)), (dw, 0, 3, 0)],
-            13: [(dx, 4, (2, 3)), (dw, 0, 3, 1)],
-            14: [(dx, 5, (0, 1)), (dx, 5, (2, 3))],
-            15.5: [(dx, 6, (0, 1))],
-        }
-        nstep = 16
-        for k in range(nstep):
-            for item in loads.get(k, []):
-                item[0](*item[1:])
-            if k >= 6 and k + 4 < nstep:
-                load_g(k + 4)
-            if k + 1 < nstep:
-                gather_psum(k + 1)
-            products(k)
-            if k >= 2:
-                feature_copy(k - 2)
-            u = (k - 3) // 2
-            finish = k % 2 == 1 and k >= 3
-            if finish:
-                token_copy(u, "S", 0, (256, 256, 256, 256, 512, 512, 512, 512)[u])
-                if (256, 256, 256, 256, 512, 512, 512, 512)[u] < HALF:
-                    token_copy(u, "V", (256, 256, 256, 256, 512, 512, 512, 512)[u], HALF)
-            for q in range(piece_count[k]):
-                if pieces:
-                    piece(*pieces[0])
-                    pieces = pieces[1:]
-            if k in (0, 2, 4):
-                sines(k // 2 + 1)
-            if k in quants:
-                quant(*quants[k])
-            if finish:
-                quant_f(u)
-                if u < G:
-                    quant_t(u)
-            if k % 2 == 0 and k >= 12:
-                quant_t((k - 4) // 2)
-            for item in products_at.get(k, []):
-                item[0](*item[1:])
-            if k >= 1:
-                mask(k - 1)
-                transposes(k - 1)
-            for item in products_at.get(k + 0.5, []):
-                item[0](*item[1:])
-            add(k)
-        mask(15)
+        piece("x", 0, 1)
+        sines(1)
+        gather_psum(0)
+        load_g(4)
+        products(0)
+        load_g(5)
+        load_raw("w", 1)
+        piece("x", 0, 2)
+        piece("x", 0, 3)
+        add(0)
+        sines(2)
+        piece("w", 0, 0)
+        gather_psum(1)
+        load_y(2, 0, F)
+        products(1)
+        piece("w", 0, 1)
+        mask(0)
+        add(1)
+        gather_psum(2)
+        load_g(6)
+        products(2)
+        load_g(7)
+        load_raw("x", 2)
+        transposes(0)
+        mask(1)
+        add(2)
+        feature_copy(0)
+        gather_psum(3)
+        quant("x", 0)
+        load_y(3, 0, F)
+        products(3)
+        transposes(1)
+        piece("w", 0, 2)
+        mask(2)
+        add(3)
+        piece("w", 0, 3)
+        feature_copy(1)
+        token_copy(0, "S", 0, 128)
+        gather_psum(4)
+        quant_f(0)
+        token_copy(0, "V", 128, 512)
+        quant("w", 0)
+        load_g(8)
+        products(4)
+        quant_t(0)
+        load_raw("x", 3)
+        load_y(0, 512, 1024)
+        piece("x", 1, 0)
+        transposes(2)
+        piece("x", 1, 1)
+        mask(3)
+        add(4)
+        piece("x", 1, 2)
+        dw(0, 5, 0, "acc")
+        feature_copy(2)
+        gather_psum(5)
+        piece("x", 1, 3)
+        quant("x", 1)
+        load_g(9)
+        products(5)
+        transposes(3)
+        sines(3)
+        mask(4)
+        add(5)
+        piece("w", 1, 0)
+        feature_copy(3)
+        token_copy(1, "S", 0, 512)
+        gather_psum(6)
+        quant_f(1)
+        load_g(10)
+        products(6)
+        quant_t(1)
+        piece("w", 1, 1)
+        transposes(4)
+        piece("w", 1, 2)
+        piece("w", 1, 3)
+        piece("x", 2, 0)
+        piece("x", 2, 1)
+        mask(5)
+        add(6)
+        piece("x", 2, 2)
+        feature_copy(4)
+        gather_psum(7)
+        dw(0, 3, 0, "acc")
+        dw(0, 2, 0, "acc")
+        load_g(11)
+        products(7)
+        quant("w", 1)
+        transposes(5)
+        mask(6)
+        add(7)
+        feature_copy(5)
+        token_copy(2, "S", 0, 512)
+        gather_psum(8)
+        quant_f(2)
+        load_g(12)
+        products(8)
+        quant_t(2)
+        piece("x", 2, 3)
+        transposes(6)
+        piece("x", 3, 0)
+        mask(7)
+        add(8)
+        quant("x", 2)
+        feature_copy(6)
+        dw(0, 2, 1, "acc")
+        gather_psum(9)
+        dw(0, 5, 1, "acc")
+        load_g(13)
+        products(9)
+        dw(0, 4, 0, "acc")
+        dw(0, 4, 1, "acc")
+        transposes(7)
+        piece("x", 3, 1)
+        piece("x", 3, 2)
+        mask(8)
+        add(9)
+        dw(0, 3, 1, "acc")
+        feature_copy(7)
+        token_copy(3, "S", 0, 512)
+        gather_psum(10)
+        quant_f(3)
+        load_g(14)
+        products(10)
+        quant_t(3)
+        dw(0, 3, 2, "acc")
+        piece("x", 3, 3)
+        dw(0, 4, 2, "acc")
+        transposes(8)
+        dw(0, 2, 2, "acc")
+        quant("x", 3)
+        mask(9)
+        add(10)
+        feature_copy(8)
+        gather_psum(11)
+        dw(0, 5, 2, "acc")
+        dw(0, 4, 3, "acc")
+        load_g(15)
+        products(11)
+        dw(0, 2, 3, "acc")
+        dw(0, 5, 3, "acc")
+        transposes(9)
+        dw_drain(0, 4, "S")
+        mask(10)
+        add(11)
+        dw_drain(0, 2, "S")
+        dw(0, 1, 0, "acc")
+        dw_drain(0, 5, "S")
+        feature_copy(9)
+        dw_store(0, 2)
+        dw(0, 0, 0, "acc")
+        dw(0, 0, 1, "acc")
+        dw(0, 3, 3, "acc")
+        token_copy(4, "S", 0, 512)
+        gather_psum(12)
+        quant_f(4)
+        products(12)
+        quant_t(4)
+        dw(0, 0, 2, "acc")
+        dw(0, 1, 1, "acc")
+        dw(0, 0, 3, "acc")
+        transposes(10)
+        dw_drain(0, 3, "S")
+        dw(0, 1, 2, "acc")
+        dw_store(0, 1)
+        mask(11)
+        add(12)
+        dw_drain(0, 0, "S")
+        feature_copy(10)
+        gather_psum(13)
+        products(13)
+        dx(0, 0, 0)
+        dx(0, 0, 1)
+        dx(0, 1, 0)
+        dx(0, 1, 1)
+        dx(0, 2, 0)
+        dx(0, 2, 1)
+        dx(0, 3, 0)
+        dx(0, 3, 1)
+        transposes(11)
+        dw(0, 1, 3, "acc")
+        mask(12)
+        add(13)
+        dx_drain(0, (0, 1), 0, 0, "S")
+        dx_drain(0, (0, 1), 0, 1, "S")
+        dx_drain(0, (0, 1), 1, 0, "S")
+        dx_drain(0, (0, 1), 1, 1, "S")
+        dx_store(0, (0, 1))
+        dx_drain(0, (2, 3), 2, 0, "S")
+        dx_drain(0, (2, 3), 2, 1, "S")
+        dx_drain(0, (2, 3), 3, 0, "S")
+        feature_copy(11)
+        dx_drain(0, (2, 3), 3, 1, "S")
+        dx_store(0, (2, 3))
+        token_copy(5, "S", 0, 512)
+        dw_drain(0, 1, "S")
+        gather_psum(14)
+        dw_store(0, 0)
+        quant_f(5)
+        dw(0, 6, 0, "acc")
+        products(14)
+        quant_t(5)
+        dw(0, 6, 1, "acc")
+        dw(0, 6, 2, "acc")
+        dw(0, 6, 3, "acc")
+        transposes(12)
+        mask(13)
+        add(14)
+        dw(1, 0, 0, "tr")
+        feature_copy(12)
+        dw_drain(0, 6, "S")
+        gather_psum(15)
+        products(15)
+        dx(1, 0, 0)
+        dw(1, 2, 0, "gp")
+        dx(1, 0, 1)
+        dx(1, 1, 0)
+        dx(1, 1, 1)
+        dx(1, 2, 0)
+        dx(1, 2, 1)
+        transposes(13)
+        dx(1, 3, 0)
+        dx(1, 3, 1)
+        mask(14)
+        dx_drain(1, (0, 1), 0, 0, "S")
+        dx_drain(1, (0, 1), 0, 1, "S")
+        dx_drain(1, (0, 1), 1, 0, "S")
+        dx_drain(1, (0, 1), 1, 1, "S")
+        dx_store(1, (0, 1))
+        dx_drain(1, (2, 3), 2, 0, "S")
+        feature_copy(13)
+        dx_drain(1, (2, 3), 2, 1, "S")
+        token_copy(6, "S", 0, 128)
+        dw(0, 7, 0, "acc")
+        dx_drain(1, (2, 3), 3, 0, "S")
+        quant_f(6)
+        dx_drain(1, (2, 3), 3, 1, "V")
+        dx_store(1, (2, 3))
+        token_copy(6, "V", 128, 512)
         quant_t(6)
-        dw_open(1, 0, 0, "gp")
-        dw_open(1, 0, 1, "gp")
+        dw(1, 1, 0, "gp")
+        transposes(14)
+        dw(1, 2, 1, "gp")
+        dx(2, 0, 0)
         feature_copy(14)
-        dx(6, (2, 3), "SV")
+        dx(2, 0, 1)
+        dx(2, 1, 0)
+        dx(2, 1, 1)
+        dx(2, 2, 0)
+        add(15)
+        dx(2, 2, 1)
+        dx(2, 3, 0)
+        dx(2, 3, 1)
+        mask(15)
+        dx_drain(2, (0, 1), 0, 0, "S")
+        dx_drain(2, (0, 1), 0, 1, "S")
+        dx_drain(2, (0, 1), 1, 0, "S")
+        dx_drain(2, (0, 1), 1, 1, "S")
         transposes(15)
-        quant_f(7, 0)
+        dx_drain(2, (2, 3), 2, 0, "S")
+        dx_store(2, (0, 1))
+        dx_drain(2, (2, 3), 2, 1, "S")
+        dx_drain(2, (2, 3), 3, 0, "S")
+        dx_drain(2, (2, 3), 3, 1, "V")
+        dx_store(2, (2, 3))
         feature_copy(15)
         token_copy(7, "S", 0, 160)
         token_copy(7, "V", 160, 512)
+        dw(0, 7, 1, "acc")
+        dw(1, 2, 2, "gp")
+        dw(1, 1, 1, "gp")
+        dw(0, 7, 2, "acc")
+        dw(1, 0, 1, "tr")
+        quant_t(7)
+        dw(1, 3, 0, "tr")
+        dw(1, 0, 2, "tr")
+        dw(0, 7, 3, "acc")
         quant_f(7, 1)
-        quant_t(7, 0, 256)
-        quant_t(7, 256, 512)
-        dx(7, (0, 2), "SV")
-        dw_open(1, 1, 0, "tr")
-        dw_open(1, 1, 1, "tr")
-        dx(7, (1, 3), "SV")
-        dw_close(1, 0, 0, "S")
-        dw_close(1, 0, 1, "V")
-        dw_close(1, 1, 0, "S")
-        dw_close(1, 1, 1, "V")
-        dw(1, 2, 0, "S")
-        dw(1, 2, 1, "V")
-        dw(1, 3, 0, "S")
-        dw(1, 3, 1, "V")
+        dw(1, 1, 2, "gp")
+        dw_drain(0, 7, "S")
+        dw_store(0, 3)
+        dw(1, 7, 0, "acc")
+        dw(1, 2, 3, "gp")
+        dw(1, 0, 3, "tr")
+        quant_f(7, 0)
+        dw_drain(1, 2, "S")
+        dw_drain(1, 0, "V")
+        dw(1, 3, 1, "tr")
+        dw(1, 1, 3, "gp")
+        dx(3, 0, 0)
+        dx(3, 0, 1)
+        dx(3, 2, 0)
+        dx(3, 2, 1)
+        dx(3, 1, 0)
+        dx(3, 1, 1)
+        dx(3, 3, 0)
+        dx(3, 3, 1)
+        dw_drain(1, 1, "S")
+        dw_store(1, 0)
+        dx_drain(3, (0, 2), 0, 0, "V")
+        dx_drain(3, (0, 2), 0, 1, "S")
+        dx_drain(3, (0, 2), 2, 0, "V")
+        dx_drain(3, (0, 2), 2, 1, "V")
+        dx_store(3, (0, 2))
+        dx_drain(3, (1, 3), 1, 0, "V")
+        dx_drain(3, (1, 3), 1, 1, "S")
+        dx_drain(3, (1, 3), 3, 0, "S")
+        dx_drain(3, (1, 3), 3, 1, "S")
+        dx_store(3, (1, 3))
+        dw(1, 6, 0, "tr")
+        dw(1, 3, 2, "tr")
+        dw(1, 6, 1, "tr")
+        dw(1, 6, 2, "tr")
+        dw(1, 4, 0, "gp")
+        dw(1, 4, 1, "gp")
+        dw(1, 6, 3, "tr")
+        dw(1, 4, 2, "gp")
+        dw(1, 4, 3, "gp")
+        dw_drain(1, 6, "S")
+        dw_drain(1, 4, "V")
+        dw(1, 3, 3, "tr")
+        dw_drain(1, 3, "S")
+        dw_store(1, 1)
+        dw(1, 7, 1, "acc")
+        dw(1, 7, 2, "acc")
+        dw(1, 7, 3, "acc")
+        dw_drain(1, 7, "S")
+        dw_store(1, 3)
+        dw(1, 5, 0, "acc")
+        dw(1, 5, 1, "acc")
+        dw(1, 5, 2, "acc")
+        dw(1, 5, 3, "acc")
+        dw_drain(1, 5, "S")
+        dw_store(1, 2)

@@ -28,8 +28,8 @@ FLOPS = 2 * 2 * T * F * E
 BYTES = T * E * 2 + F * E * 2 + T * F * 4 + T * F * 2 + T * E * 4 + F * E * 4
 
 EXACT = 8
-FCENG = "SSSSSSSSSSSSSSSV"
-UNITS = ((0, 0), (0, 1), (0, 2), (0, 3), (1, 0), (1, 1), (1, 2), (1, 3))
+CHUNKS = ((0, 0), (0, 1), (0, 2), (0, 3), (1, 0), (2, 0), (3, 0), (1, 1), (1, 2), (1, 3), (2, 1), (3, 1), (2, 2), (2, 3), (3, 2), (3, 3))
+AT = {c: i for i, c in enumerate(CHUNKS)}
 PSUM_BUFS = {"gp": 2, "tr": 2, "acc": 4}
 
 
@@ -65,32 +65,28 @@ def tile_weightlinearattention_pa_v_kernel(tc, x, w, bias, y, grad_out, out_0, o
         nc.gpsimd.iota(npos[:], pattern=[[256, 4], [1, 2]], base=0, channel_multiplier=2,
                        allow_small_or_imprecise_dtypes=True)
 
-        y_tiles = []
-        for g in range(G):
-            yt = keep.tile([P, PACK, F], F32, name=f"y{g}", align_bytes=64)
-            y_tiles.append(yt)
         xc = keep.tile([P, G, E], U32, name="xc", align_bytes=64)
         xs = keep.tile([P, G, E], U8, name="xs", align_bytes=64)
         wc = keep.tile([P, 2, E], U32, name="wc", align_bytes=64)
         ws = keep.tile([P, 2, E], U8, name="ws", align_bytes=64)
-        tcod = keep.tile([P, 2, G, HALF], U32, name="tcod", align_bytes=64)
-        tsc = keep.tile([P, 2, G, HALF], U8, name="tsc", align_bytes=64)
-        facod = keep.tile([P, G, 512], U32, name="facod", align_bytes=64)
-        fasc = keep.tile([P, G, 512], U8, name="fasc", align_bytes=64)
+        tcod = keep.tile([P, 4, G, 256], U32, name="tcod", align_bytes=64)
+        tsc = keep.tile([P, 4, G, 256], U8, name="tsc", align_bytes=64)
+        fcod = keep.tile([P, G, 2, 512], U32, name="fcod", align_bytes=64)
+        fsc = keep.tile([P, G, 2, 512], U8, name="fsc", align_bytes=64)
 
-        g_tiles = {}
-        raws = {}
-        inters = {}
+        g_tiles, y_tiles, raws, inters = {}, {}, {}, {}
 
         def load_g(k):
-            u, c = k // 2, k % 2
-            hf, g = UNITS[u]
-            gt = stream.tile([P, HH, 2 * D], BF16, name="gt", tag="gt", bufs=6, align_bytes=64)
-            nc.sync.dma_start(out=gt[:], in_=g_view[c, g, :, hf * HH:(hf + 1) * HH, :])
+            g, h = CHUNKS[k]
+            gt = stream.tile([P, 2, 2, 2 * D], BF16, name="gt", tag="gt", bufs=6, align_bytes=64)
+            for c in range(2):
+                nc.sync.dma_start(out=gt[:, c], in_=g_view[c, g, :, 2 * h:2 * h + 2, :])
             g_tiles[k] = gt
 
-        def load_y(g, lo, hi):
-            nc.sync.dma_start(out=y_tiles[g][:, :, lo:hi], in_=y_view[g, :, :, lo:hi])
+        def load_y(g, hf):
+            yt = stream.tile([P, PACK, HALF], F32, name="yt", tag="yt", bufs=5, align_bytes=64)
+            nc.sync.dma_start(out=yt[:], in_=y_view[g, :, :, hf * HALF:(hf + 1) * HALF])
+            y_tiles[(g, hf)] = yt
 
         def load_raw(which, i):
             rt = stream.tile([P, PACK, E], BF16, name="raw", tag="raw", bufs=3, align_bytes=64)
@@ -143,13 +139,26 @@ def tile_weightlinearattention_pa_v_kernel(tc, x, w, bias, y, grad_out, out_0, o
             nc.scalar.activation(out=sin_v[:, :, :, 0], in_=reduced[:, 0, r], func=ACT.Sin, scale=tau)
             nc.scalar.activation(out=sin_v[:, :, :, 1], in_=reduced[:, 0, r], func=ACT.Sin, scale=-tau)
 
-        def piece(which, i, q):
+        spread = {}
+
+        def weight_spread(i, q):
+            wps = psum.tile([P, 256, PACK], BF16, name="wps", tag="acc", bufs=PSUM_BUFS["acc"])
+            for half in range(2):
+                cols = slice(q * 256 + half * 128, q * 256 + half * 128 + 128)
+                nc.tensor.matmul(out=wps[:, half * 128:half * 128 + 128, :], lhsT=ident_bf[:],
+                                 rhs=raws[("w", i)][:, :, cols].rearrange("p j e -> p e j"), start=True, stop=True)
+            spread[(i, q)] = wps
+
+        def piece(which, i, q, eng):
             if q == 0:
                 it = stream.tile([P, E, PACK], BF16, name="inter", tag="inter", bufs=2, align_bytes=64)
                 inters[(which, i)] = it
             cols = slice(q * 256, (q + 1) * 256)
-            nc.scalar.copy(out=inters[(which, i)][:, cols, :].rearrange("p (c i) j -> p c j i", i=4),
-                           in_=raws[(which, i)][:, :, cols].rearrange("p j (c i) -> p c j i", i=4))
+            if which == "w":
+                drain(inters[(which, i)][:, cols, :].rearrange("p e j -> p (e j)"), spread[(i, q)][:].rearrange("p e j -> p (e j)"), eng)
+                return
+            drain(inters[(which, i)][:, cols, :].rearrange("p (c i) j -> p c j i", i=4),
+                  raws[(which, i)][:, :, cols].rearrange("p j (c i) -> p c j i", i=4), eng)
 
         def quant(which, i):
             codes, scales = (xc, xs) if which == "x" else (wc, ws)
@@ -159,498 +168,535 @@ def tile_weightlinearattention_pa_v_kernel(tc, x, w, bias, y, grad_out, out_0, o
         def drain(dst, acc, eng):
             if eng == "V":
                 nc.vector.tensor_copy(out=dst, in_=acc)
+            elif eng == "G":
+                nc.gpsimd.tensor_scalar(out=dst, in0=acc, scalar1=1.0, scalar2=0.0, op0=ALU.mult, op1=ALU.add)
             else:
                 nc.scalar.copy(out=dst, in_=acc)
 
-        gps, ms, drs, dzs, trs, dzfs, dzis, fbs = {}, {}, {}, {}, {}, {}, {}, {}
+        gps, ms, drs, dzs, trs, dzfs, dzis = {}, {}, {}, {}, {}, {}, {}
 
         def gather_psum(k):
             gp = psum.tile([P, 1024], BF16, name="gp", tag="gp", bufs=PSUM_BUFS["gp"])
-            gt = g_tiles[k][:].rearrange("p h r -> p (h r)")
+            gt = g_tiles[k][:].rearrange("p c h r -> p (c h r)")
             for q in range(2):
                 nc.tensor.matmul(out=gp[:, 512 * q:512 * q + 512], lhsT=ident_bf[:], rhs=gt[:, 512 * q:512 * q + 512],
                                  start=True, stop=True)
             gps[k] = gp
 
         def products(k):
-            g = UNITS[k // 2][1]
+            g = CHUNKS[k][0]
             m1 = stream.tile([P, 1024], F32, name="m1", tag="m1", bufs=2, align_bytes=64)
             m2 = stream.tile([P, 1024], F32, name="m2", tag="m2", bufs=2, align_bytes=64)
             gp = gps[k][:]
             nc.vector.tensor_tensor(
-                out=m1[:].rearrange("p (s h d) -> p h s d", s=2, h=HH),
-                in0=gp.rearrange("p (h s d) -> p h s d", h=HH, s=2),
-                in1=cos_t[:, 2 * g:2 * g + 2].unsqueeze(1).to_broadcast([P, HH, 2, D]), op=ALU.mult)
+                out=m1[:].rearrange("p (s b d) -> p b s d", s=2, b=4),
+                in0=gp.rearrange("p (b s d) -> p b s d", b=4, s=2),
+                in1=cos_t[:, 2 * g:2 * g + 2].unsqueeze(1).to_broadcast([P, 4, 2, D]), op=ALU.mult)
             nc.vector.tensor_tensor(
-                out=m2[:].rearrange("p (s h i e) -> p h s i e", s=2, h=HH, e=2),
-                in0=gp.rearrange("p (h s i e) -> p h s i e", h=HH, s=2, e=2)[:, :, :, :, ::-1],
-                in1=sin_t[:, 2 * g:2 * g + 2].rearrange("p s (i e) -> p s i e", e=2).unsqueeze(1).to_broadcast([P, HH, 2, NPAIR, 2]),
+                out=m2[:].rearrange("p (s b i e) -> p b s i e", s=2, b=4, e=2),
+                in0=gp.rearrange("p (b s i e) -> p b s i e", b=4, s=2, e=2)[:, :, :, :, ::-1],
+                in1=sin_t[:, 2 * g:2 * g + 2].rearrange("p s (i e) -> p s i e", e=2).unsqueeze(1).to_broadcast([P, 4, 2, NPAIR, 2]),
                 op=ALU.mult)
             ms[k] = (m1, m2)
 
-        def add(k):
-            dr = stream.tile([P, 2, HALF], F32, name="dr", tag="dr", bufs=1, align_bytes=64)
+        def add(k, eng):
+            dr = stream.tile([P, PACK, 256], F32, name="dr", tag="dr", bufs=1, align_bytes=64)
             m1, m2 = ms[k]
-            eng = nc.vector if k >= 16 - 1 else nc.gpsimd
-            eng.tensor_tensor(out=dr[:].rearrange("p s f -> p (s f)"), in0=m1[:], in1=m2[:], op=ALU.add)
+            (nc.vector if eng == "V" else nc.gpsimd).tensor_tensor(out=dr[:].rearrange("p j f -> p (j f)"), in0=m1[:], in1=m2[:],
+                                                                   op=ALU.add)
             drs[k] = dr
 
         def mask(k):
-            u, c = k // 2, k % 2
-            hf, g = UNITS[u]
-            if c == 0:
-                dz = stream.tile([P, PACK, HALF], BF16, name="dz", tag="dz", bufs=2, align_bytes=64)
-                dzs[u] = dz
-            nc.vector.scalar_tensor_tensor(
-                out=dzs[u][:, c:PACK:2, :], in0=y_tiles[g][:, c:PACK:2, hf * HALF:(hf + 1) * HALF], scalar=0.0,
-                in1=drs[k][:], op0=ALU.is_gt, op1=ALU.mult)
+            g, h = CHUNKS[k]
+            if (g, h // 2) not in dzs:
+                dz = stream.tile([P, PACK, HALF], BF16, name="dz", tag="dz", bufs=5, align_bytes=64)
+                dzs[(g, h // 2)] = dz
+            cols = slice(h % 2 * 256, h % 2 * 256 + 256)
+            nc.vector.scalar_tensor_tensor(out=dzs[(g, h // 2)][:, :, cols], in0=y_tiles[(g, h // 2)][:, :, cols], scalar=0.0,
+                                           in1=drs[k][:], op0=ALU.is_gt, op1=ALU.mult)
 
-        def transposes(k):
-            u, c = k // 2, k % 2
-            words = dzs[u][:].bitcast(F32)
+        def token_copy(k, eng):
+            g, h = CHUNKS[k]
+            cols = slice(h % 2 * 256, h % 2 * 256 + 256)
+            dzi = stream.tile([P, 256, PACK], BF16, name="dzi", tag="dzi", bufs=2, align_bytes=64)
+            drain(dzi[:].rearrange("p (c i) j -> p c j i", i=4),
+                  dzs[(g, h // 2)][:, :, cols].rearrange("p j (c i) -> p c j i", i=4), eng)
+            dzis[k] = dzi
+
+        def quant_t(k):
+            g, h = CHUNKS[k]
+            nc.vector.quantize_mx(out=tcod[:, h, g, :].bitcast(E5M2X4), scales=tsc[:, h, g, :],
+                                  in_=dzis[k][:].rearrange("p f j -> p (f j)"))
+
+        def transposes(g, hf, b):
+            words = dzs[(g, hf)][:].bitcast(F32)
             tr = psum.tile([P, 2, 2, P], F32, name="tr", tag="tr", bufs=PSUM_BUFS["tr"])
-            for s in range(2):
+            for jj in range(2):
                 for v in range(2):
-                    nc.tensor.transpose(tr[:, s, v, :], words[:, 2 * s + c, v::2], ident_f[:])
-            trs[k] = tr
+                    nc.tensor.transpose(tr[:, jj, v, :], words[:, 2 * b + jj, v::2], ident_f[:])
+            trs[(g, hf, b)] = tr
 
-        def feature_copy(k):
-            u, c = k // 2, k % 2
-            if c == 0:
+        def feature_copy(g, hf, b, eng):
+            if (g, hf) not in dzfs:
                 dzf = stream.tile([P, PACK, P, PACK], BF16, name="dzf", tag="dzf", bufs=2, align_bytes=64)
-                dzfs[u] = dzf
-            drain(dzfs[u][:].bitcast(F32)[:, c:PACK:2], trs[k][:].rearrange("p s v r -> p s r v"), FCENG[k])
+                dzfs[(g, hf)] = dzf
+            drain(dzfs[(g, hf)][:].bitcast(F32)[:, 2 * b:2 * b + 2], trs[(g, hf, b)][:].rearrange("p j v r -> p j r v"), eng)
 
-        def token_copy(u, eng, lo=None, hi=None):
-            if u not in dzis:
-                dzi = stream.tile([P, HALF, PACK], BF16, name="dzi", tag="dzi", bufs=1, align_bytes=64)
-                dzis[u] = dzi
-            if lo is None:
-                lo, hi = (0, 256) if eng == "S" else (256, 512)
-            dst = dzis[u][:, lo:hi, :].rearrange("p (c i) j -> p c j i", i=4)
-            srcv = dzs[u][:, :, lo:hi].rearrange("p j (c i) -> p c j i", i=4)
-            if eng == "S":
-                nc.scalar.copy(out=dst, in_=srcv)
-            else:
-                nc.vector.tensor_copy(out=dst, in_=srcv)
-
-        def quant_f(u, c=None):
-            hf, g = UNITS[u]
-            if c is not None:
-                if g not in fbs:
-                    fbc = stream.tile([P, 512], U32, name="fbc", tag="fbc", bufs=2, align_bytes=64)
-                    fbs_ = stream.tile([P, 512], U8, name="fbs", tag="fbs", bufs=2, align_bytes=64)
-                    fbs[g] = (fbc, fbs_)
-                for s in range(2):
-                    j = 2 * s + c
-                    cols = slice(j * P, j * P + P)
-                    nc.vector.quantize_mx(out=fbs[g][0][:, cols].bitcast(E5M2X4), scales=fbs[g][1][:, cols],
-                                          in_=dzfs[u][:, j].rearrange("p r t -> p (r t)"))
-                return
-            if hf == 0:
-                codes, scales = facod[:, g, :], fasc[:, g, :]
-            else:
-                fbc = stream.tile([P, 512], U32, name="fbc", tag="fbc", bufs=2, align_bytes=64)
-                fbs_ = stream.tile([P, 512], U8, name="fbs", tag="fbs", bufs=2, align_bytes=64)
-                fbs[g] = (fbc, fbs_)
-                codes, scales = fbc[:], fbs_[:]
-            nc.vector.quantize_mx(out=codes.bitcast(E5M2X4), scales=scales,
-                                  in_=dzfs[u][:].rearrange("p j r t -> p (j r t)"))
-
-        def quant_t(u, lo=0, hi=HALF):
-            hf, g = UNITS[u]
-            nc.vector.quantize_mx(out=tcod[:, hf, g, lo:hi].bitcast(E5M2X4), scales=tsc[:, hf, g, lo:hi],
-                                  in_=dzis[u][:, lo:hi].rearrange("p f j -> p (f j)"))
+        def quant_f(g, hf):
+            nc.vector.quantize_mx(out=fcod[:, g, hf, :].bitcast(E5M2X4), scales=fsc[:, g, hf, :],
+                                  in_=dzfs[(g, hf)][:].rearrange("p j r t -> p (j r t)"))
 
         dx_stage, dx_acc, dw_stage, dw_acc = {}, {}, {}, {}
 
-        def dx(g, j, eh):
+        def dx(g, b, hf, pool="acc"):
+            j, eh = b // 2, b % 2
             cols = slice(j * P, (j + 1) * P)
             ecols = slice(eh * 512, eh * 512 + 512)
-            acc = psum.tile([P, 512], F32, name="acc", tag="acc", bufs=PSUM_BUFS["acc"])
-            dx_acc[(g, j, eh)] = acc
-            nc.tensor.matmul_mx(out=acc[:], lhsT=facod[:, g, cols].bitcast(E5M2X4), lhsT_scale=fasc[:, g, cols],
-                                rhs=wc[:, 0, ecols].bitcast(E4M3X4), rhs_scale=ws[:, 0, ecols], start=True, stop=False)
-            nc.tensor.matmul_mx(out=acc[:], lhsT=fbs[g][0][:, cols].bitcast(E5M2X4), lhsT_scale=fbs[g][1][:, cols],
-                                rhs=wc[:, 1, ecols].bitcast(E4M3X4), rhs_scale=ws[:, 1, ecols], start=False, stop=True)
+            if hf == 0:
+                acc = psum.tile([P, 512], F32, name="acc", tag=pool, bufs=PSUM_BUFS[pool])
+                dx_acc[(g, b)] = acc
+            nc.tensor.matmul_mx(out=dx_acc[(g, b)][:], lhsT=fcod[:, g, hf, cols].bitcast(E5M2X4), lhsT_scale=fsc[:, g, hf, cols],
+                                rhs=wc[:, hf, ecols].bitcast(E4M3X4), rhs_scale=ws[:, hf, ecols], start=(hf == 0), stop=(hf == 1))
 
-        def dx_drain(g, js, j, eh, eng):
-            if (g, js) not in dx_stage:
+        def dx_drain(g, b, eng):
+            if (g, b // 4) not in dx_stage:
                 ost = stream.tile([P, 2, E], F32, name="ost", tag="raw", bufs=3, align_bytes=64)
-                dx_stage[(g, js)] = ost
-            drain(dx_stage[(g, js)][:, js.index(j), eh * 512:eh * 512 + 512], dx_acc[(g, j, eh)][:], eng)
+                dx_stage[(g, b // 4)] = ost
+            eh = b % 2
+            drain(dx_stage[(g, b // 4)][:, b // 2 % 2, eh * 512:eh * 512 + 512], dx_acc[(g, b)][:], eng)
 
-        def dx_store(g, js):
-            nc.sync.dma_start(out=o0_view[g, :, js[0]:js[1] + 1:js[1] - js[0], :], in_=dx_stage[(g, js)][:])
+        def dx_store_row(g, j):
+            nc.sync.dma_start(out=o0_view[g, :, j, :], in_=dx_stage[(g, j // 2)][:, j % 2])
 
-        def dw(hf, b, g, pool):
-            m, eh = b // 2, b % 2
-            cols = slice(m * P, (m + 1) * P)
-            ecols = slice(eh * 512, eh * 512 + 512)
-            if g == 0:
+        def dx_store(g, q):
+            nc.sync.dma_start(out=o0_view[g, :, 2 * q:2 * q + 2, :], in_=dx_stage[(g, q)][:])
+
+        def dw(h, b, r, pool):
+            order = sorted(range(G), key=lambda gg: AT[(gg, h)])
+            g = order[r]
+            cols = slice(b // 2 * P, b // 2 * P + P)
+            ecols = slice(b % 2 * 512, b % 2 * 512 + 512)
+            if r == 0:
                 accw = psum.tile([P, 512], F32, name="accw", tag=pool, bufs=PSUM_BUFS[pool])
-                dw_acc[(hf, b)] = accw
-            nc.tensor.matmul_mx(out=dw_acc[(hf, b)][:], lhsT=tcod[:, hf, g, cols].bitcast(E5M2X4),
-                                lhsT_scale=tsc[:, hf, g, cols], rhs=xc[:, g, ecols].bitcast(E4M3X4),
-                                rhs_scale=xs[:, g, ecols], start=(g == 0), stop=(g == G - 1))
+                dw_acc[(h, b)] = accw
+            nc.tensor.matmul_mx(out=dw_acc[(h, b)][:], lhsT=tcod[:, h, g, cols].bitcast(E5M2X4), lhsT_scale=tsc[:, h, g, cols],
+                                rhs=xc[:, g, ecols].bitcast(E4M3X4), rhs_scale=xs[:, g, ecols], start=(r == 0), stop=(r == G - 1))
 
-        def dw_drain(hf, b, eng):
-            m, eh = b // 2, b % 2
-            if (hf, m // 2) not in dw_stage:
+        def dw_drain(h, b, eng):
+            if h not in dw_stage:
                 ostw = stream.tile([P, 2, E], F32, name="ostw", tag="inter", bufs=2, align_bytes=64)
-                dw_stage[(hf, m // 2)] = ostw
-            drain(dw_stage[(hf, m // 2)][:, m % 2, eh * 512:eh * 512 + 512], dw_acc[(hf, b)][:], eng)
+                dw_stage[h] = ostw
+            eh = b % 2
+            drain(dw_stage[h][:, b // 2, eh * 512:eh * 512 + 512], dw_acc[(h, b)][:], eng)
 
-        def dw_store(hf, m):
-            nc.sync.dma_start(out=o1_view[hf * 4 + m], in_=dw_stage[(hf, m // 2)][:, m % 2])
+        def dw_store(h, mm):
+            nc.sync.dma_start(out=o1_view[2 * h + mm], in_=dw_stage[h][:, mm])
 
-        load_g(0)
-        load_g(1)
-        load_raw("x", 0)
-        load_y(0, 0, 512)
-        load_g(2)
-        load_g(3)
-        load_raw("w", 0)
-        load_y(1, 0, F)
-        load_raw("x", 1)
         frequencies()
         make_identity(nc, ident_bf[:])
         make_identity(nc, ident_f[:])
         turns_rows(0, 2)
-        sines(0)
-        piece("x", 0, 0)
-        turns_rows(2, 8)
-        piece("x", 0, 1)
-        sines(1)
-        gather_psum(0)
+        load_g(0)
+        load_raw("x", 0)
+        load_g(1)
         load_g(4)
+        load_y(0, 0)
+        sines(0)
+        turns_rows(2, 4)
+        gather_psum(0)
+        load_g(2)
+        load_g(3)
         products(0)
-        load_g(5)
+        sines(1)
         load_raw("w", 1)
-        piece("x", 0, 2)
-        piece("x", 0, 3)
-        add(0)
-        sines(2)
-        piece("w", 0, 0)
+        piece("x", 0, 0, "S")
         gather_psum(1)
-        load_y(2, 0, F)
+        piece("x", 0, 3, "G")
+        piece("x", 0, 1, "S")
         products(1)
-        piece("w", 0, 1)
-        mask(0)
-        add(1)
-        gather_psum(2)
-        load_g(6)
-        products(2)
-        load_g(7)
-        load_raw("x", 2)
-        transposes(0)
-        mask(1)
-        add(2)
-        feature_copy(0)
-        gather_psum(3)
-        quant("x", 0)
-        load_y(3, 0, F)
-        products(3)
-        transposes(1)
-        piece("w", 0, 2)
-        mask(2)
-        add(3)
-        piece("w", 0, 3)
-        feature_copy(1)
-        token_copy(0, "S", 0, 128)
         gather_psum(4)
-        quant_f(0)
-        token_copy(0, "V", 128, 512)
-        quant("w", 0)
-        load_g(8)
-        products(4)
-        quant_t(0)
-        load_raw("x", 3)
-        load_y(0, 512, 1024)
-        piece("x", 1, 0)
-        transposes(2)
-        piece("x", 1, 1)
-        mask(3)
-        add(4)
-        piece("x", 1, 2)
-        dw(0, 5, 0, "acc")
-        feature_copy(2)
-        gather_psum(5)
-        piece("x", 1, 3)
-        quant("x", 1)
+        load_y(0, 1)
+        piece("x", 0, 2, "S")
+        add(0, "G")
+        turns_rows(4, 8)
         load_g(9)
-        products(5)
-        transposes(3)
+        gather_psum(2)
+        load_raw("w", 0)
+        mask(0)
+        sines(2)
         sines(3)
-        mask(4)
-        add(5)
-        piece("w", 1, 0)
-        feature_copy(3)
-        token_copy(1, "S", 0, 512)
-        gather_psum(6)
-        quant_f(1)
-        load_g(10)
-        products(6)
-        quant_t(1)
-        piece("w", 1, 1)
-        transposes(4)
-        piece("w", 1, 2)
-        piece("w", 1, 3)
-        piece("x", 2, 0)
-        piece("x", 2, 1)
-        mask(5)
-        add(6)
-        piece("x", 2, 2)
-        feature_copy(4)
-        gather_psum(7)
-        dw(0, 3, 0, "acc")
-        dw(0, 2, 0, "acc")
-        load_g(11)
-        products(7)
-        quant("w", 1)
-        transposes(5)
-        mask(6)
-        add(7)
-        feature_copy(5)
-        token_copy(2, "S", 0, 512)
-        gather_psum(8)
-        quant_f(2)
-        load_g(12)
-        products(8)
-        quant_t(2)
-        piece("x", 2, 3)
-        transposes(6)
-        piece("x", 3, 0)
-        mask(7)
-        add(8)
-        quant("x", 2)
-        feature_copy(6)
-        dw(0, 2, 1, "acc")
-        gather_psum(9)
-        dw(0, 5, 1, "acc")
-        load_g(13)
-        products(9)
-        dw(0, 4, 0, "acc")
-        dw(0, 4, 1, "acc")
-        transposes(7)
-        piece("x", 3, 1)
-        piece("x", 3, 2)
-        mask(8)
-        add(9)
-        dw(0, 3, 1, "acc")
-        feature_copy(7)
-        token_copy(3, "S", 0, 512)
-        gather_psum(10)
-        quant_f(3)
-        load_g(14)
-        products(10)
-        quant_t(3)
-        dw(0, 3, 2, "acc")
-        piece("x", 3, 3)
-        dw(0, 4, 2, "acc")
-        transposes(8)
-        dw(0, 2, 2, "acc")
-        quant("x", 3)
-        mask(9)
-        add(10)
-        feature_copy(8)
-        gather_psum(11)
-        dw(0, 5, 2, "acc")
-        dw(0, 4, 3, "acc")
-        load_g(15)
-        products(11)
-        dw(0, 2, 3, "acc")
-        dw(0, 5, 3, "acc")
-        transposes(9)
-        dw_drain(0, 4, "S")
-        mask(10)
-        add(11)
-        dw_drain(0, 2, "S")
-        dw(0, 1, 0, "acc")
-        dw_drain(0, 5, "S")
-        feature_copy(9)
-        dw_store(0, 2)
+        quant("x", 0)
+        token_copy(0, "S")
+        load_g(7)
+        products(2)
+        add(1, "G")
+        weight_spread(1, 0)
+        load_g(5)
+        weight_spread(1, 1)
+        piece("w", 1, 0, "S")
+        weight_spread(1, 2)
+        piece("w", 1, 1, "S")
+        weight_spread(1, 3)
+        piece("w", 1, 2, "S")
+        load_g(6)
+        quant_t(0)
+        load_raw("x", 2)
+        gather_psum(3)
+        piece("w", 1, 3, "S")
+        mask(1)
         dw(0, 0, 0, "acc")
-        dw(0, 0, 1, "acc")
-        dw(0, 3, 3, "acc")
-        token_copy(4, "S", 0, 512)
-        gather_psum(12)
-        quant_f(4)
-        products(12)
-        quant_t(4)
-        dw(0, 0, 2, "acc")
-        dw(0, 1, 1, "acc")
-        dw(0, 0, 3, "acc")
-        transposes(10)
-        dw_drain(0, 3, "S")
-        dw(0, 1, 2, "acc")
-        dw_store(0, 1)
-        mask(11)
-        add(12)
-        dw_drain(0, 0, "S")
-        feature_copy(10)
-        gather_psum(13)
-        products(13)
-        dx(0, 0, 0)
-        dx(0, 0, 1)
-        dx(0, 1, 0)
-        dx(0, 1, 1)
-        dx(0, 2, 0)
+        dw(0, 1, 0, "acc")
+        quant("w", 1)
+        token_copy(1, "S")
+        transposes(0, 0, 0)
+        load_y(3, 0)
+        transposes(0, 0, 1)
+        products(3)
+        add(2, "G")
+        feature_copy(0, 0, 0, "S")
+        weight_spread(0, 0)
+        feature_copy(0, 0, 1, "S")
+        weight_spread(0, 1)
+        piece("w", 0, 0, "S")
+        load_y(1, 0)
+        weight_spread(0, 2)
+        piece("w", 0, 1, "S")
+        quant_f(0, 0)
+        gather_psum(5)
+        piece("w", 0, 2, "S")
+        mask(2)
+        weight_spread(0, 3)
+        piece("w", 0, 3, "S")
+        quant_t(1)
+        load_raw("x", 1)
+        products(4)
+        add(3, "G")
+        token_copy(2, "S")
+        piece("x", 2, 0, "S")
+        load_y(2, 0)
+        gather_psum(6)
+        quant_t(2)
+        mask(3)
+        piece("x", 2, 1, "S")
+        quant("w", 0)
+        transposes(0, 1, 0)
+        token_copy(3, "S")
+        transposes(0, 1, 1)
+        load_raw("x", 3)
+        products(5)
+        add(4, "G")
+        dx(0, 2, 0, "acc")
+        feature_copy(0, 1, 0, "S")
+        dx(0, 4, 0, "acc")
+        piece("x", 2, 2, "S")
+        load_g(8)
+        feature_copy(0, 1, 1, "S")
+        gather_psum(7)
+        quant_t(3)
+        load_g(11)
+        mask(4)
+        piece("x", 2, 3, "S")
+        load_y(3, 1)
+        quant_f(0, 1)
+        token_copy(4, "S")
+        products(6)
+        add(5, "G")
         dx(0, 2, 1)
-        dx(0, 3, 0)
-        dx(0, 3, 1)
-        transposes(11)
-        dw(0, 1, 3, "acc")
-        mask(12)
-        add(13)
-        dx_drain(0, (0, 1), 0, 0, "S")
-        dx_drain(0, (0, 1), 0, 1, "S")
-        dx_drain(0, (0, 1), 1, 0, "S")
-        dx_drain(0, (0, 1), 1, 1, "S")
-        dx_store(0, (0, 1))
-        dx_drain(0, (2, 3), 2, 0, "S")
-        dx_drain(0, (2, 3), 2, 1, "S")
-        dx_drain(0, (2, 3), 3, 0, "S")
-        feature_copy(11)
-        dx_drain(0, (2, 3), 3, 1, "S")
-        dx_store(0, (2, 3))
-        token_copy(5, "S", 0, 512)
-        dw_drain(0, 1, "S")
-        gather_psum(14)
-        dw_store(0, 0)
-        quant_f(5)
-        dw(0, 6, 0, "acc")
-        products(14)
+        dx(0, 4, 1)
+        dx_drain(0, 4, "S")
+        piece("x", 1, 0, "S")
+        load_g(14)
+        dx(0, 0, 0, "acc")
+        dx(0, 0, 1)
+        gather_psum(9)
+        load_g(15)
+        quant_t(4)
+        mask(5)
+        piece("x", 1, 1, "S")
+        load_y(1, 1)
+        quant("x", 2)
+        token_copy(5, "S")
+        products(7)
+        add(6, "G")
+        piece("x", 1, 2, "S")
+        piece("x", 1, 3, "S")
+        gather_psum(8)
         quant_t(5)
-        dw(0, 6, 1, "acc")
-        dw(0, 6, 2, "acc")
-        dw(0, 6, 3, "acc")
-        transposes(12)
-        mask(13)
-        add(14)
-        dw(1, 0, 0, "tr")
-        feature_copy(12)
-        dw_drain(0, 6, "S")
-        gather_psum(15)
-        products(15)
-        dx(1, 0, 0)
-        dw(1, 2, 0, "gp")
-        dx(1, 0, 1)
-        dx(1, 1, 0)
-        dx(1, 1, 1)
-        dx(1, 2, 0)
-        dx(1, 2, 1)
-        transposes(13)
-        dx(1, 3, 0)
-        dx(1, 3, 1)
-        mask(14)
-        dx_drain(1, (0, 1), 0, 0, "S")
-        dx_drain(1, (0, 1), 0, 1, "S")
-        dx_drain(1, (0, 1), 1, 0, "S")
-        dx_drain(1, (0, 1), 1, 1, "S")
-        dx_store(1, (0, 1))
-        dx_drain(1, (2, 3), 2, 0, "S")
-        feature_copy(13)
-        dx_drain(1, (2, 3), 2, 1, "S")
-        token_copy(6, "S", 0, 128)
-        dw(0, 7, 0, "acc")
-        dx_drain(1, (2, 3), 3, 0, "S")
-        quant_f(6)
-        dx_drain(1, (2, 3), 3, 1, "V")
-        dx_store(1, (2, 3))
-        token_copy(6, "V", 128, 512)
+        mask(6)
+        piece("x", 3, 0, "S")
+        quant("x", 1)
+        dx_drain(0, 0, "S")
+        token_copy(6, "S")
+        dx(0, 1, 0, "acc")
+        products(8)
+        add(7, "G")
+        dw(0, 0, 1, "acc")
+        dx(0, 1, 1)
+        dw(0, 0, 2, "acc")
+        dx_drain(0, 1, "S")
+        dw(0, 1, 1, "acc")
+        dw(0, 1, 2, "acc")
+        dx_drain(0, 2, "S")
+        dx(0, 3, 0, "acc")
+        dx(0, 3, 1)
+        piece("x", 3, 1, "S")
         quant_t(6)
-        dw(1, 1, 0, "gp")
-        transposes(14)
-        dw(1, 2, 1, "gp")
-        dx(2, 0, 0)
-        feature_copy(14)
-        dx(2, 0, 1)
-        dx(2, 1, 0)
-        dx(2, 1, 1)
-        dx(2, 2, 0)
-        add(15)
-        dx(2, 2, 1)
-        dx(2, 3, 0)
-        dx(2, 3, 1)
-        mask(15)
-        dx_drain(2, (0, 1), 0, 0, "S")
-        dx_drain(2, (0, 1), 0, 1, "S")
-        dx_drain(2, (0, 1), 1, 0, "S")
-        dx_drain(2, (0, 1), 1, 1, "S")
-        transposes(15)
-        dx_drain(2, (2, 3), 2, 0, "S")
-        dx_store(2, (0, 1))
-        dx_drain(2, (2, 3), 2, 1, "S")
-        dx_drain(2, (2, 3), 3, 0, "S")
-        dx_drain(2, (2, 3), 3, 1, "V")
-        dx_store(2, (2, 3))
-        feature_copy(15)
-        token_copy(7, "S", 0, 160)
-        token_copy(7, "V", 160, 512)
-        dw(0, 7, 1, "acc")
-        dw(1, 2, 2, "gp")
-        dw(1, 1, 1, "gp")
-        dw(0, 7, 2, "acc")
-        dw(1, 0, 1, "tr")
+        gather_psum(11)
+        mask(7)
+        dx(0, 5, 0, "acc")
+        dx_drain(0, 3, "S")
+        dx(0, 5, 1)
+        products(9)
+        load_y(2, 1)
+        add(8, "G")
+        transposes(1, 0, 0)
+        load_g(10)
+        dx_drain(0, 5, "S")
+        load_g(13)
+        dx_store(0, 0)
+        transposes(1, 0, 1)
+        token_copy(7, "S")
+        dx(0, 6, 0, "acc")
+        dx(0, 7, 0, "acc")
+        dx(0, 6, 1)
+        feature_copy(1, 0, 0, "S")
+        dx(0, 7, 1)
         quant_t(7)
-        dw(1, 3, 0, "tr")
-        dw(1, 0, 2, "tr")
-        dw(0, 7, 3, "acc")
-        quant_f(7, 1)
-        dw(1, 1, 2, "gp")
-        dw_drain(0, 7, "S")
-        dw_store(0, 3)
-        dw(1, 7, 0, "acc")
-        dw(1, 2, 3, "gp")
-        dw(1, 0, 3, "tr")
-        quant_f(7, 0)
-        dw_drain(1, 2, "S")
-        dw_drain(1, 0, "V")
-        dw(1, 3, 1, "tr")
-        dw(1, 1, 3, "gp")
-        dx(3, 0, 0)
-        dx(3, 0, 1)
-        dx(3, 2, 0)
-        dx(3, 2, 1)
-        dx(3, 1, 0)
-        dx(3, 1, 1)
-        dx(3, 3, 0)
-        dx(3, 3, 1)
+        gather_psum(14)
+        dx_drain(0, 6, "S")
+        load_g(12)
+        mask(8)
+        feature_copy(1, 0, 1, "S")
+        dw(0, 2, 0, "acc")
+        dx_drain(0, 7, "S")
+        dw(0, 2, 1, "acc")
+        quant_f(1, 0)
+        dw(0, 2, 2, "acc")
+        token_copy(8, "S")
+        dx_store(0, 1)
+        products(11)
+        add(9, "G")
+        dw(0, 3, 0, "acc")
+        dw(0, 3, 1, "acc")
+        dw(0, 3, 2, "acc")
+        piece("x", 3, 2, "S")
+        gather_psum(10)
+        quant_t(8)
+        piece("x", 3, 3, "S")
+        mask(9)
+        quant("x", 3)
+        token_copy(9, "S")
+        transposes(1, 1, 0)
+        transposes(1, 1, 1)
+        products(10)
+        add(11, "G")
+        dw(0, 0, 3, "acc")
+        feature_copy(1, 1, 0, "S")
+        dw(0, 1, 3, "acc")
+        dw_drain(0, 0, "S")
+        dw(0, 2, 3, "acc")
+        dw(0, 3, 3, "acc")
+        feature_copy(1, 1, 1, "S")
+        dx(1, 3, 0, "acc")
+        dw_drain(0, 1, "S")
+        gather_psum(12)
+        quant_f(1, 1)
+        dw_drain(0, 2, "S")
+        dw_store(0, 0)
+        mask(11)
+        dx(1, 5, 0, "acc")
+        dw_drain(0, 3, "S")
+        dx(1, 0, 0, "acc")
+        dx(1, 3, 1)
+        dw_store(0, 1)
+        dx(1, 1, 0, "acc")
+        quant_t(9)
+        token_copy(11, "S")
+        transposes(3, 0, 0)
+        products(12)
+        add(10, "G")
+        transposes(3, 0, 1)
+        dx(1, 0, 1)
+        feature_copy(3, 0, 0, "S")
+        dx(1, 1, 1)
+        dx_drain(1, 0, "S")
+        dx(1, 5, 1)
+        feature_copy(3, 0, 1, "S")
+        dx(1, 2, 0, "acc")
+        quant_t(11)
+        gather_psum(13)
+        mask(10)
+        dx_drain(1, 1, "S")
+        dx(1, 2, 1)
+        dx_drain(1, 3, "S")
+        dx(1, 4, 0, "acc")
+        quant_f(3, 0)
+        transposes(2, 0, 0)
+        dx_drain(1, 2, "S")
+        products(13)
+        add(12, "G")
+        token_copy(10, "S")
+        transposes(2, 0, 1)
+        dx_store(1, 0)
+        dx(1, 4, 1)
+        dx(1, 6, 0, "acc")
+        dx(1, 7, 0, "acc")
+        feature_copy(2, 0, 0, "S")
+        dx(1, 6, 1)
+        dx(1, 7, 1)
+        dx_drain(1, 4, "S")
+        gather_psum(15)
+        quant_t(10)
+        feature_copy(2, 0, 1, "S")
+        mask(12)
+        dw(1, 0, 0, "acc")
+        dx_drain(1, 5, "S")
+        dw(1, 0, 1, "acc")
+        dx_drain(1, 6, "S")
+        dw(1, 1, 0, "acc")
+        quant_f(2, 0)
+        dw(1, 0, 2, "acc")
+        dx_drain(1, 7, "S")
+        dw(1, 1, 1, "acc")
+        products(14)
+        add(13, "G")
+        dw(1, 2, 0, "acc")
+        token_copy(12, "S")
+        dx_store(1, 1)
+        dw(1, 1, 2, "acc")
+        dw(1, 2, 1, "acc")
+        dw(1, 3, 0, "acc")
+        dw(1, 2, 2, "acc")
+        dw(1, 3, 1, "acc")
+        dw(1, 0, 3, "acc")
+        dw(1, 3, 2, "acc")
+        dw_drain(1, 0, "S")
+        quant_t(12)
+        dw(1, 1, 3, "acc")
+        dw(1, 2, 3, "acc")
+        mask(13)
         dw_drain(1, 1, "S")
+        dx(2, 0, 0, "acc")
+        dw(1, 3, 3, "acc")
+        dw_drain(1, 2, "S")
         dw_store(1, 0)
-        dx_drain(3, (0, 2), 0, 0, "V")
-        dx_drain(3, (0, 2), 0, 1, "S")
-        dx_drain(3, (0, 2), 2, 0, "V")
-        dx_drain(3, (0, 2), 2, 1, "V")
-        dx_store(3, (0, 2))
-        dx_drain(3, (1, 3), 1, 0, "V")
-        dx_drain(3, (1, 3), 1, 1, "S")
-        dx_drain(3, (1, 3), 3, 0, "S")
-        dx_drain(3, (1, 3), 3, 1, "S")
-        dx_store(3, (1, 3))
-        dw(1, 6, 0, "tr")
-        dw(1, 3, 2, "tr")
-        dw(1, 6, 1, "tr")
-        dw(1, 6, 2, "tr")
-        dw(1, 4, 0, "gp")
-        dw(1, 4, 1, "gp")
-        dw(1, 6, 3, "tr")
-        dw(1, 4, 2, "gp")
-        dw(1, 4, 3, "gp")
-        dw_drain(1, 6, "S")
-        dw_drain(1, 4, "V")
-        dw(1, 3, 3, "tr")
+        dx(2, 3, 0, "acc")
+        products(15)
+        add(14, "G")
+        transposes(2, 1, 0)
+        token_copy(13, "S")
+        transposes(2, 1, 1)
+        dw(3, 1, 0, "acc")
+        feature_copy(2, 1, 0, "S")
+        dw(3, 1, 1, "acc")
         dw_drain(1, 3, "S")
+        dw(3, 0, 0, "gp")
+        quant_t(13)
+        dw(2, 1, 0, "gp")
+        feature_copy(2, 1, 1, "S")
         dw_store(1, 1)
-        dw(1, 7, 1, "acc")
-        dw(1, 7, 2, "acc")
-        dw(1, 7, 3, "acc")
-        dw_drain(1, 7, "S")
-        dw_store(1, 3)
-        dw(1, 5, 0, "acc")
-        dw(1, 5, 1, "acc")
-        dw(1, 5, 2, "acc")
-        dw(1, 5, 3, "acc")
-        dw_drain(1, 5, "S")
-        dw_store(1, 2)
+        mask(14)
+        dw(3, 1, 2, "acc")
+        dw(2, 1, 1, "gp")
+        dw(3, 0, 1, "gp")
+        dw(2, 1, 2, "gp")
+        quant_f(2, 1)
+        dw(3, 0, 2, "gp")
+        token_copy(14, "S")
+        dw(2, 0, 0, "acc")
+        add(15, "V")
+        dx(2, 0, 1)
+        dw(2, 0, 1, "acc")
+        dx(2, 3, 1)
+        dx_drain(2, 0, "S")
+        dw(2, 0, 2, "acc")
+        quant_t(14)
+        dx(2, 1, 0, "acc")
+        dx_drain(2, 3, "S")
+        mask(15)
+        dw(2, 0, 3, "acc")
+        dx(2, 1, 1)
+        dw_drain(2, 0, "S")
+        dx(2, 2, 0, "acc")
+        dw(2, 1, 3, "gp")
+        dx_drain(2, 1, "S")
+        transposes(3, 1, 0)
+        dw_drain(2, 1, "V")
+        token_copy(15, "S")
+        transposes(3, 1, 1)
+        feature_copy(3, 1, 0, "V")
+        dw_store(2, 0)
+        dx(2, 2, 1)
+        feature_copy(3, 1, 1, "V")
+        dx(2, 4, 0, "acc")
+        dx_drain(2, 2, "S")
+        dx(2, 5, 0, "acc")
+        quant_t(15)
+        dx(2, 4, 1)
+        dx_store(2, 0)
+        quant_f(3, 1)
+        dx(2, 5, 1)
+        dx_drain(2, 4, "S")
+        dw(3, 0, 3, "gp")
+        dw(3, 1, 3, "acc")
+        dw_drain(3, 0, "S")
+        dx_drain(2, 5, "V")
+        dw(3, 2, 0, "acc")
+        dw(3, 3, 0, "gp")
+        dw(3, 2, 1, "acc")
+        dw_drain(3, 1, "S")
+        dw(3, 3, 1, "gp")
+        dw(3, 2, 2, "acc")
+        dw_store(3, 0)
+        dw(3, 3, 2, "gp")
+        dw(3, 2, 3, "acc")
+        dw(3, 3, 3, "gp")
+        dw_drain(3, 2, "S")
+        dx(2, 6, 0, "acc")
+        dw_drain(3, 3, "V")
+        dx(2, 7, 0, "acc")
+        dx(2, 6, 1)
+        dw_store(3, 1)
+        dx(2, 7, 1)
+        dx_drain(2, 6, "V")
+        dw(2, 2, 0, "tr")
+        dx_drain(2, 7, "S")
+        dw(2, 3, 0, "gp")
+        dw(2, 2, 1, "tr")
+        dx_store(2, 1)
+        dw(2, 3, 1, "gp")
+        dw(2, 2, 2, "tr")
+        dw(2, 3, 2, "gp")
+        dw(2, 2, 3, "tr")
+        dw(2, 3, 3, "gp")
+        dw_drain(2, 2, "V")
+        dx(3, 0, 0, "acc")
+        dw_drain(2, 3, "S")
+        dx(3, 1, 0, "acc")
+        dx(3, 0, 1)
+        dw_store(2, 1)
+        dx(3, 1, 1)
+        dx_drain(3, 0, "S")
+        dx(3, 2, 0, "acc")
+        dx(3, 3, 0, "gp")
+        dx_drain(3, 1, "V")
+        dx(3, 2, 1)
+        dx(3, 3, 1)
+        dx_drain(3, 2, "V")
+        dx(3, 4, 0, "gp")
+        dx_store_row(3, 0)
+        dx_drain(3, 3, "S")
+        dx(3, 5, 0, "tr")
+        dx(3, 4, 1)
+        dx_store_row(3, 1)
+        dx(3, 5, 1)
+        dx_drain(3, 4, "V")
+        dx(3, 6, 0, "gp")
+        dx(3, 6, 1)
+        dx_drain(3, 5, "S")
+        dx(3, 7, 0, "gp")
+        dx_drain(3, 6, "V")
+        dx_store_row(3, 2)
+        dx(3, 7, 1)
+        dx_drain(3, 7, "V")
+        dx_store_row(3, 3)

import math
from contextlib import ExitStack

import concourse.mybir as mybir
from concourse.masks import make_identity

F32 = mybir.dt.float32
BF16 = mybir.dt.bfloat16
I32 = mybir.dt.int32
U32 = mybir.dt.uint32
U8 = mybir.dt.uint8
E4M3X4 = mybir.dt.float8_e4m3fn_x4
E5M2X4 = mybir.dt.float8_e5m2_x4
ALU = mybir.AluOpType
ACT = mybir.ActivationFunctionType

L, B, E, H, D = 1024, 2, 1024, 8, 128
F = H * D
T = L * B
P = 128
PACK = 4
G = 4
HALF = F // 2
HH = H // 2
NPAIR = D // 2

FLOPS = 2 * 2 * T * F * E
BYTES = T * E * 2 + F * E * 2 + T * F * 4 + T * F * 2 + T * E * 4 + F * E * 4

EXACT = 8
CHUNKS = ((0, 0), (0, 1), (0, 2), (0, 3), (1, 0), (2, 0), (3, 0), (1, 1), (1, 2), (1, 3), (2, 1), (3, 1), (2, 2), (2, 3), (3, 2), (3, 3))
AT = {c: i for i, c in enumerate(CHUNKS)}
PSUM_BUFS = {"gp": 2, "tr": 2, "acc": 4}


def tile_weightlinearattention_pa_v_kernel(tc, x, w, bias, y, grad_out, out_0, out_1):
    nc = tc.nc
    with ExitStack() as ctx:
        keep = ctx.enter_context(tc.tile_pool(name="keep", bufs=1))
        stream = ctx.enter_context(tc.tile_pool(name="stream", bufs=2))
        psum = ctx.enter_context(tc.psum_pool(name="psum", bufs=2))
        ctx.enter_context(tc.manual_schedule())

        x_view = x.rearrange("n c e -> (n c) e").rearrange("(g p j) e -> g p j e", p=P, j=PACK)
        w_view = w.rearrange("(g p j) e -> g p j e", p=P, j=PACK)
        y_view = y.rearrange("n c f -> (n c) f").rearrange("(g p j) f -> g p j f", p=P, j=PACK)
        g_view = grad_out.rearrange("c h (g p s) d -> c g p h (s d)", p=P, s=2)
        o0_view = out_0.rearrange("n c e -> (n c) e").rearrange("(g p j) e -> g p j e", p=P, j=PACK)
        o1_view = out_1.rearrange("(m p) e -> m p e", p=P)

        ident_bf = keep.tile([P, P], BF16, name="ident_bf", align_bytes=64)
        ident_f = keep.tile([P, P], F32, name="ident_f", align_bytes=64)
        npos = keep.tile([P, 8], F32, name="npos", align_bytes=64)
        one = keep.tile([P, 1], F32, name="one", align_bytes=64)
        warm = keep.tile([P, 1], F32, name="warm", align_bytes=64)
        quarter = keep.tile([P, 1], F32, name="quarter", align_bytes=64)
        freq = keep.tile([P, NPAIR], F32, name="freq", align_bytes=64)
        rest = keep.tile([P, EXACT], F32, name="rest", align_bytes=64)
        turns = keep.tile([P, 8, NPAIR], F32, name="turns", align_bytes=64)
        whole = keep.tile([P, 8, NPAIR], I32, name="whole", align_bytes=64)
        cos_t = keep.tile([P, 8, D], F32, name="cos_t", align_bytes=64)
        sin_t = keep.tile([P, 8, D], F32, name="sin_t", align_bytes=64)

        nc.vector.memset(one[:], 1.0)
        nc.gpsimd.iota(npos[:], pattern=[[256, 4], [1, 2]], base=0, channel_multiplier=2,
                       allow_small_or_imprecise_dtypes=True)

        xc = keep.tile([P, G, E], U32, name="xc", align_bytes=64)
        xs = keep.tile([P, G, E], U8, name="xs", align_bytes=64)
        wc = keep.tile([P, 2, E], U32, name="wc", align_bytes=64)
        ws = keep.tile([P, 2, E], U8, name="ws", align_bytes=64)
        tcod = keep.tile([P, 4, G, 256], U32, name="tcod", align_bytes=64)
        tsc = keep.tile([P, 4, G, 256], U8, name="tsc", align_bytes=64)
        fcod = keep.tile([P, G, 2, 512], U32, name="fcod", align_bytes=64)
        fsc = keep.tile([P, G, 2, 512], U8, name="fsc", align_bytes=64)

        g_tiles, y_tiles, raws, inters = {}, {}, {}, {}

        def load_g(k):
            g, h = CHUNKS[k]
            gt = stream.tile([P, 2, 2, 2 * D], BF16, name="gt", tag="gt", bufs=6, align_bytes=64)
            for c in range(2):
                nc.sync.dma_start(out=gt[:, c], in_=g_view[c, g, :, 2 * h:2 * h + 2, :])
            g_tiles[k] = gt

        def load_y(g, hf):
            yt = stream.tile([P, PACK, HALF], F32, name="yt", tag="yt", bufs=5, align_bytes=64)
            nc.sync.dma_start(out=yt[:], in_=y_view[g, :, :, hf * HALF:(hf + 1) * HALF])
            y_tiles[(g, hf)] = yt

        def load_raw(which, i):
            rt = stream.tile([P, PACK, E], BF16, name="raw", tag="raw", bufs=3, align_bytes=64)
            nc.sync.dma_start(out=rt[:], in_=(x_view if which == "x" else w_view)[i])
            raws[(which, i)] = rt

        def frequencies():
            nc.scalar.activation(out=warm[:], in_=one[:], func=ACT.Sin)
            nc.vector.tensor_scalar(out=quarter[:], in0=one[:], scalar1=math.pi / 2.0, scalar2=None, op0=ALU.mult)
            theta = [10000.0 ** (-2.0 * i / D) / (2.0 * math.pi) for i in range(NPAIR)]
            for i in range(EXACT):
                scale = 2.0 ** (13 - math.floor(math.log2(theta[i])))
                hi = math.floor(theta[i] * scale) / scale
                nc.gpsimd.memset(freq[:, i:i + 1], hi)
                nc.scalar.activation(out=rest[:, i:i + 1], in_=one[:], func=ACT.Copy, scale=theta[i] - hi)
            nc.vector.tensor_scalar(out=freq[:, EXACT:EXACT + 1], in0=one[:], scalar1=theta[EXACT], scalar2=None, op0=ALU.mult)
            have = 1
            while EXACT + have < NPAIR:
                n = min(have, NPAIR - EXACT - have)
                nc.vector.tensor_scalar(out=freq[:, EXACT + have:EXACT + have + n], in0=freq[:, EXACT:EXACT + n],
                                        scalar1=10000.0 ** (-2.0 * have / D), scalar2=None, op0=ALU.mult)
                have += n

        reduced = keep.tile([P, 2, 8, NPAIR], F32, name="reduced", align_bytes=64)

        def turns_rows(lo, hi):
            n = hi - lo
            r = slice(lo, hi)
            fine = stream.tile([P, 2, n, EXACT], F32, name="fine", tag="m2", bufs=2, align_bytes=64)
            nc.vector.tensor_tensor(out=turns[:, r], in0=npos[:, r].unsqueeze(2).to_broadcast([P, n, NPAIR]),
                                    in1=freq[:].unsqueeze(1).to_broadcast([P, n, NPAIR]), op=ALU.mult)
            nc.vector.tensor_tensor(out=fine[:, 0], in0=npos[:, r].unsqueeze(2).to_broadcast([P, n, EXACT]),
                                    in1=rest[:].unsqueeze(1).to_broadcast([P, n, EXACT]), op=ALU.mult)
            nc.vector.tensor_copy(out=whole[:, r, EXACT:], in_=turns[:, r, EXACT:])
            nc.vector.tensor_tensor(out=fine[:, 1], in0=turns[:, r, 0:EXACT], in1=fine[:, 0], op=ALU.add)
            nc.vector.tensor_copy(out=whole[:, r, 0:EXACT], in_=fine[:, 1])
            nc.vector.scalar_tensor_tensor(out=reduced[:, 0, r], in0=whole[:, r], scalar=-1.0, in1=turns[:, r],
                                           op0=ALU.mult, op1=ALU.add)
            nc.vector.tensor_tensor(out=reduced[:, 0, r, 0:EXACT], in0=reduced[:, 0, r, 0:EXACT], in1=fine[:, 0], op=ALU.add)
            nc.vector.scalar_tensor_tensor(out=reduced[:, 1, r], in0=reduced[:, 0, r], scalar=0.25, in1=reduced[:, 0, r],
                                           op0=ALU.is_gt, op1=ALU.subtract)

        def sines(g):
            tau = 2.0 * math.pi
            r = slice(2 * g, 2 * g + 2)
            sin_v = sin_t[:, r].rearrange("p r (i e) -> p r i e", e=2)
            nc.scalar.activation(out=cos_t[:, r].rearrange("p r (i e) -> p r i e", e=2),
                                 in_=reduced[:, 1, r].unsqueeze(3).to_broadcast([P, 2, NPAIR, 2]), func=ACT.Sin,
                                 scale=-tau, bias=quarter[:])
            nc.scalar.activation(out=sin_v[:, :, :, 0], in_=reduced[:, 0, r], func=ACT.Sin, scale=tau)
            nc.scalar.activation(out=sin_v[:, :, :, 1], in_=reduced[:, 0, r], func=ACT.Sin, scale=-tau)

        spread = {}

        def weight_spread(i, q):
            wps = psum.tile([P, 256, PACK], BF16, name="wps", tag="acc", bufs=PSUM_BUFS["acc"])
            for half in range(2):
                cols = slice(q * 256 + half * 128, q * 256 + half * 128 + 128)
                nc.tensor.matmul(out=wps[:, half * 128:half * 128 + 128, :], lhsT=ident_bf[:],
                                 rhs=raws[("w", i)][:, :, cols].rearrange("p j e -> p e j"), start=True, stop=True)
            spread[(i, q)] = wps

        def piece(which, i, q, eng):
            if q == 0:
                it = stream.tile([P, E, PACK], BF16, name="inter", tag="inter", bufs=2, align_bytes=64)
                inters[(which, i)] = it
            cols = slice(q * 256, (q + 1) * 256)
            if which == "w":
                drain(inters[(which, i)][:, cols, :].rearrange("p e j -> p (e j)"), spread[(i, q)][:].rearrange("p e j -> p (e j)"), eng)
                return
            drain(inters[(which, i)][:, cols, :].rearrange("p (c i) j -> p c j i", i=4),
                  raws[(which, i)][:, :, cols].rearrange("p j (c i) -> p c j i", i=4), eng)

        def quant(which, i):
            codes, scales = (xc, xs) if which == "x" else (wc, ws)
            nc.vector.quantize_mx(out=codes[:, i, :].bitcast(E4M3X4), scales=scales[:, i, :],
                                  in_=inters[(which, i)][:].rearrange("p e j -> p (e j)"))

        def drain(dst, acc, eng):
            if eng == "V":
                nc.vector.tensor_copy(out=dst, in_=acc)
            elif eng == "G":
                nc.gpsimd.tensor_scalar(out=dst, in0=acc, scalar1=1.0, scalar2=0.0, op0=ALU.mult, op1=ALU.add)
            else:
                nc.scalar.copy(out=dst, in_=acc)

        gps, ms, drs, dzs, trs, dzfs, dzis = {}, {}, {}, {}, {}, {}, {}

        def gather_psum(k):
            gp = psum.tile([P, 1024], BF16, name="gp", tag="gp", bufs=PSUM_BUFS["gp"])
            gt = g_tiles[k][:].rearrange("p c h r -> p (c h r)")
            for q in range(2):
                nc.tensor.matmul(out=gp[:, 512 * q:512 * q + 512], lhsT=ident_bf[:], rhs=gt[:, 512 * q:512 * q + 512],
                                 start=True, stop=True)
            gps[k] = gp

        def products(k):
            g = CHUNKS[k][0]
            m1 = stream.tile([P, 1024], F32, name="m1", tag="m1", bufs=2, align_bytes=64)
            m2 = stream.tile([P, 1024], F32, name="m2", tag="m2", bufs=2, align_bytes=64)
            gp = gps[k][:]
            nc.vector.tensor_tensor(
                out=m1[:].rearrange("p (s b d) -> p b s d", s=2, b=4),
                in0=gp.rearrange("p (b s d) -> p b s d", b=4, s=2),
                in1=cos_t[:, 2 * g:2 * g + 2].unsqueeze(1).to_broadcast([P, 4, 2, D]), op=ALU.mult)
            nc.vector.tensor_tensor(
                out=m2[:].rearrange("p (s b i e) -> p b s i e", s=2, b=4, e=2),
                in0=gp.rearrange("p (b s i e) -> p b s i e", b=4, s=2, e=2)[:, :, :, :, ::-1],
                in1=sin_t[:, 2 * g:2 * g + 2].rearrange("p s (i e) -> p s i e", e=2).unsqueeze(1).to_broadcast([P, 4, 2, NPAIR, 2]),
                op=ALU.mult)
            ms[k] = (m1, m2)

        def add(k, eng):
            dr = stream.tile([P, PACK, 256], F32, name="dr", tag="dr", bufs=1, align_bytes=64)
            m1, m2 = ms[k]
            (nc.vector if eng == "V" else nc.gpsimd).tensor_tensor(out=dr[:].rearrange("p j f -> p (j f)"), in0=m1[:], in1=m2[:],
                                                                   op=ALU.add)
            drs[k] = dr

        def mask(k):
            g, h = CHUNKS[k]
            if (g, h // 2) not in dzs:
                dz = stream.tile([P, PACK, HALF], BF16, name="dz", tag="dz", bufs=5, align_bytes=64)
                dzs[(g, h // 2)] = dz
            cols = slice(h % 2 * 256, h % 2 * 256 + 256)
            nc.vector.scalar_tensor_tensor(out=dzs[(g, h // 2)][:, :, cols], in0=y_tiles[(g, h // 2)][:, :, cols], scalar=0.0,
                                           in1=drs[k][:], op0=ALU.is_gt, op1=ALU.mult)

        def token_copy(k, eng):
            g, h = CHUNKS[k]
            cols = slice(h % 2 * 256, h % 2 * 256 + 256)
            dzi = stream.tile([P, 256, PACK], BF16, name="dzi", tag="dzi", bufs=2, align_bytes=64)
            drain(dzi[:].rearrange("p (c i) j -> p c j i", i=4),
                  dzs[(g, h // 2)][:, :, cols].rearrange("p j (c i) -> p c j i", i=4), eng)
            dzis[k] = dzi

        def quant_t(k):
            g, h = CHUNKS[k]
            nc.vector.quantize_mx(out=tcod[:, h, g, :].bitcast(E5M2X4), scales=tsc[:, h, g, :],
                                  in_=dzis[k][:].rearrange("p f j -> p (f j)"))

        def transposes(g, hf, b):
            words = dzs[(g, hf)][:].bitcast(F32)
            tr = psum.tile([P, 2, 2, P], F32, name="tr", tag="tr", bufs=PSUM_BUFS["tr"])
            for jj in range(2):
                for v in range(2):
                    nc.tensor.transpose(tr[:, jj, v, :], words[:, 2 * b + jj, v::2], ident_f[:])
            trs[(g, hf, b)] = tr

        def feature_copy(g, hf, b, eng):
            if (g, hf) not in dzfs:
                dzf = stream.tile([P, PACK, P, PACK], BF16, name="dzf", tag="dzf", bufs=2, align_bytes=64)
                dzfs[(g, hf)] = dzf
            drain(dzfs[(g, hf)][:].bitcast(F32)[:, 2 * b:2 * b + 2], trs[(g, hf, b)][:].rearrange("p j v r -> p j r v"), eng)

        def quant_f(g, hf):
            nc.vector.quantize_mx(out=fcod[:, g, hf, :].bitcast(E5M2X4), scales=fsc[:, g, hf, :],
                                  in_=dzfs[(g, hf)][:].rearrange("p j r t -> p (j r t)"))

        dx_stage, dx_acc, dw_stage, dw_acc = {}, {}, {}, {}

        def dx(g, b, hf, pool="acc"):
            j, eh = b // 2, b % 2
            cols = slice(j * P, (j + 1) * P)
            ecols = slice(eh * 512, eh * 512 + 512)
            if hf == 0:
                acc = psum.tile([P, 512], F32, name="acc", tag=pool, bufs=PSUM_BUFS[pool])
                dx_acc[(g, b)] = acc
            nc.tensor.matmul_mx(out=dx_acc[(g, b)][:], lhsT=fcod[:, g, hf, cols].bitcast(E5M2X4), lhsT_scale=fsc[:, g, hf, cols],
                                rhs=wc[:, hf, ecols].bitcast(E4M3X4), rhs_scale=ws[:, hf, ecols], start=(hf == 0), stop=(hf == 1))

        def dx_drain(g, b, eng):
            if (g, b // 4) not in dx_stage:
                ost = stream.tile([P, 2, E], F32, name="ost", tag="raw", bufs=3, align_bytes=64)
                dx_stage[(g, b // 4)] = ost
            eh = b % 2
            drain(dx_stage[(g, b // 4)][:, b // 2 % 2, eh * 512:eh * 512 + 512], dx_acc[(g, b)][:], eng)

        def dx_store_row(g, j):
            nc.sync.dma_start(out=o0_view[g, :, j, :], in_=dx_stage[(g, j // 2)][:, j % 2])

        def dx_store(g, q):
            nc.sync.dma_start(out=o0_view[g, :, 2 * q:2 * q + 2, :], in_=dx_stage[(g, q)][:])

        def dw(h, b, r, pool):
            order = sorted(range(G), key=lambda gg: AT[(gg, h)])
            g = order[r]
            cols = slice(b // 2 * P, b // 2 * P + P)
            ecols = slice(b % 2 * 512, b % 2 * 512 + 512)
            if r == 0:
                accw = psum.tile([P, 512], F32, name="accw", tag=pool, bufs=PSUM_BUFS[pool])
                dw_acc[(h, b)] = accw
            nc.tensor.matmul_mx(out=dw_acc[(h, b)][:], lhsT=tcod[:, h, g, cols].bitcast(E5M2X4), lhsT_scale=tsc[:, h, g, cols],
                                rhs=xc[:, g, ecols].bitcast(E4M3X4), rhs_scale=xs[:, g, ecols], start=(r == 0), stop=(r == G - 1))

        def dw_drain(h, b, eng):
            if h not in dw_stage:
                ostw = stream.tile([P, 2, E], F32, name="ostw", tag="inter", bufs=2, align_bytes=64)
                dw_stage[h] = ostw
            eh = b % 2
            drain(dw_stage[h][:, b // 2, eh * 512:eh * 512 + 512], dw_acc[(h, b)][:], eng)

        def dw_store(h, mm):
            nc.sync.dma_start(out=o1_view[2 * h + mm], in_=dw_stage[h][:, mm])

        frequencies()
        make_identity(nc, ident_bf[:])
        make_identity(nc, ident_f[:])
        turns_rows(0, 2)
        load_g(0)
        load_raw("x", 0)
        load_g(1)
        load_g(4)
        load_y(0, 0)
        sines(0)
        turns_rows(2, 4)
        gather_psum(0)
        load_g(2)
        load_g(3)
        products(0)
        sines(1)
        load_raw("w", 1)
        piece("x", 0, 0, "S")
        gather_psum(1)
        piece("x", 0, 3, "G")
        piece("x", 0, 1, "S")
        products(1)
        gather_psum(4)
        load_y(0, 1)
        piece("x", 0, 2, "S")
        add(0, "G")
        turns_rows(4, 8)
        load_g(9)
        gather_psum(2)
        load_raw("w", 0)
        mask(0)
        sines(2)
        sines(3)
        quant("x", 0)
        token_copy(0, "S")
        load_g(7)
        products(2)
        add(1, "G")
        weight_spread(1, 0)
        load_g(5)
        weight_spread(1, 1)
        piece("w", 1, 0, "S")
        weight_spread(1, 2)
        piece("w", 1, 1, "S")
        weight_spread(1, 3)
        piece("w", 1, 2, "S")
        load_g(6)
        quant_t(0)
        load_raw("x", 2)
        gather_psum(3)
        piece("w", 1, 3, "S")
        mask(1)
        dw(0, 0, 0, "acc")
        dw(0, 1, 0, "acc")
        quant("w", 1)
        token_copy(1, "S")
        transposes(0, 0, 0)
        load_y(3, 0)
        transposes(0, 0, 1)
        products(3)
        add(2, "G")
        feature_copy(0, 0, 0, "S")
        weight_spread(0, 0)
        feature_copy(0, 0, 1, "S")
        weight_spread(0, 1)
        piece("w", 0, 0, "S")
        load_y(1, 0)
        weight_spread(0, 2)
        piece("w", 0, 1, "S")
        quant_f(0, 0)
        gather_psum(5)
        piece("w", 0, 2, "S")
        mask(2)
        weight_spread(0, 3)
        piece("w", 0, 3, "S")
        quant_t(1)
        load_raw("x", 1)
        products(4)
        add(3, "G")
        token_copy(2, "S")
        piece("x", 2, 0, "S")
        load_y(2, 0)
        gather_psum(6)
        quant_t(2)
        mask(3)
        piece("x", 2, 1, "S")
        quant("w", 0)
        transposes(0, 1, 0)
        token_copy(3, "S")
        transposes(0, 1, 1)
        load_raw("x", 3)
        products(5)
        add(4, "G")
        dx(0, 2, 0, "acc")
        feature_copy(0, 1, 0, "S")
        dx(0, 4, 0, "acc")
        piece("x", 2, 2, "S")
        load_g(8)
        feature_copy(0, 1, 1, "S")
        gather_psum(7)
        quant_t(3)
        load_g(11)
        mask(4)
        piece("x", 2, 3, "S")
        load_y(3, 1)
        quant_f(0, 1)
        token_copy(4, "S")
        products(6)
        add(5, "G")
        dx(0, 2, 1)
        dx(0, 4, 1)
        dx_drain(0, 4, "S")
        piece("x", 1, 0, "S")
        load_g(14)
        dx(0, 0, 0, "acc")
        dx(0, 0, 1)
        gather_psum(9)
        load_g(15)
        quant_t(4)
        mask(5)
        piece("x", 1, 1, "S")
        load_y(1, 1)
        quant("x", 2)
        token_copy(5, "S")
        products(7)
        add(6, "G")
        piece("x", 1, 2, "S")
        piece("x", 1, 3, "S")
        gather_psum(8)
        quant_t(5)
        mask(6)
        piece("x", 3, 0, "S")
        quant("x", 1)
        dx_drain(0, 0, "S")
        token_copy(6, "S")
        dx(0, 1, 0, "acc")
        products(8)
        add(7, "G")
        dw(0, 0, 1, "acc")
        dx(0, 1, 1)
        dw(0, 0, 2, "acc")
        dx_drain(0, 1, "S")
        dw(0, 1, 1, "acc")
        dw(0, 1, 2, "acc")
        dx_drain(0, 2, "S")
        dx(0, 3, 0, "acc")
        dx(0, 3, 1)
        piece("x", 3, 1, "S")
        quant_t(6)
        gather_psum(11)
        mask(7)
        dx(0, 5, 0, "acc")
        dx_drain(0, 3, "S")
        dx(0, 5, 1)
        products(9)
        load_y(2, 1)
        add(8, "G")
        transposes(1, 0, 0)
        load_g(10)
        dx_drain(0, 5, "S")
        load_g(13)
        dx_store(0, 0)
        transposes(1, 0, 1)
        token_copy(7, "S")
        dx(0, 6, 0, "acc")
        dx(0, 7, 0, "acc")
        dx(0, 6, 1)
        feature_copy(1, 0, 0, "S")
        dx(0, 7, 1)
        quant_t(7)
        gather_psum(14)
        dx_drain(0, 6, "S")
        load_g(12)
        mask(8)
        feature_copy(1, 0, 1, "S")
        dw(0, 2, 0, "acc")
        dx_drain(0, 7, "S")
        dw(0, 2, 1, "acc")
        quant_f(1, 0)
        dw(0, 2, 2, "acc")
        token_copy(8, "S")
        dx_store(0, 1)
        products(11)
        add(9, "G")
        dw(0, 3, 0, "acc")
        dw(0, 3, 1, "acc")
        dw(0, 3, 2, "acc")
        piece("x", 3, 2, "S")
        gather_psum(10)
        quant_t(8)
        piece("x", 3, 3, "S")
        mask(9)
        quant("x", 3)
        token_copy(9, "S")
        transposes(1, 1, 0)
        transposes(1, 1, 1)
        products(10)
        add(11, "G")
        dw(0, 0, 3, "acc")
        feature_copy(1, 1, 0, "S")
        dw(0, 1, 3, "acc")
        dw_drain(0, 0, "S")
        dw(0, 2, 3, "acc")
        dw(0, 3, 3, "acc")
        feature_copy(1, 1, 1, "S")
        dx(1, 3, 0, "acc")
        dw_drain(0, 1, "S")
        gather_psum(12)
        quant_f(1, 1)
        dw_drain(0, 2, "S")
        dw_store(0, 0)
        mask(11)
        dx(1, 5, 0, "acc")
        dw_drain(0, 3, "S")
        dx(1, 0, 0, "acc")
        dx(1, 3, 1)
        dw_store(0, 1)
        dx(1, 1, 0, "acc")
        quant_t(9)
        token_copy(11, "S")
        transposes(3, 0, 0)
        products(12)
        add(10, "G")
        transposes(3, 0, 1)
        dx(1, 0, 1)
        feature_copy(3, 0, 0, "S")
        dx(1, 1, 1)
        dx_drain(1, 0, "S")
        dx(1, 5, 1)
        feature_copy(3, 0, 1, "S")
        dx(1, 2, 0, "acc")
        quant_t(11)
        gather_psum(13)
        mask(10)
        dx_drain(1, 1, "S")
        dx(1, 2, 1)
        dx_drain(1, 3, "S")
        dx(1, 4, 0, "acc")
        quant_f(3, 0)
        transposes(2, 0, 0)
        dx_drain(1, 2, "S")
        products(13)
        add(12, "G")
        token_copy(10, "S")
        transposes(2, 0, 1)
        dx_store(1, 0)
        dx(1, 4, 1)
        dx(1, 6, 0, "acc")
        dx(1, 7, 0, "acc")
        feature_copy(2, 0, 0, "S")
        dx(1, 6, 1)
        dx(1, 7, 1)
        dx_drain(1, 4, "S")
        gather_psum(15)
        quant_t(10)
        feature_copy(2, 0, 1, "S")
        mask(12)
        dw(1, 0, 0, "acc")
        dx_drain(1, 5, "S")
        dw(1, 0, 1, "acc")
        dx_drain(1, 6, "S")
        dw(1, 1, 0, "acc")
        quant_f(2, 0)
        dw(1, 0, 2, "acc")
        dx_drain(1, 7, "S")
        dw(1, 1, 1, "acc")
        products(14)
        add(13, "G")
        dw(1, 2, 0, "acc")
        token_copy(12, "S")
        dx_store(1, 1)
        dw(1, 1, 2, "acc")
        dw(1, 2, 1, "acc")
        dw(1, 3, 0, "acc")
        dw(1, 2, 2, "acc")
        dw(1, 3, 1, "acc")
        dw(1, 0, 3, "acc")
        dw(1, 3, 2, "acc")
        dw_drain(1, 0, "S")
        quant_t(12)
        dw(1, 1, 3, "acc")
        dw(1, 2, 3, "acc")
        mask(13)
        dw_drain(1, 1, "S")
        dx(2, 0, 0, "acc")
        dw(1, 3, 3, "acc")
        dw_drain(1, 2, "S")
        dw_store(1, 0)
        dx(2, 3, 0, "acc")
        products(15)
        add(14, "G")
        transposes(2, 1, 0)
        token_copy(13, "S")
        transposes(2, 1, 1)
        dw(3, 1, 0, "acc")
        feature_copy(2, 1, 0, "S")
        dw(3, 1, 1, "acc")
        dw_drain(1, 3, "S")
        dw(3, 0, 0, "gp")
        quant_t(13)
        dw(2, 1, 0, "gp")
        feature_copy(2, 1, 1, "S")
        dw_store(1, 1)
        mask(14)
        dw(3, 1, 2, "acc")
        dw(2, 1, 1, "gp")
        dw(3, 0, 1, "gp")
        dw(2, 1, 2, "gp")
        quant_f(2, 1)
        dw(3, 0, 2, "gp")
        token_copy(14, "S")
        dw(2, 0, 0, "acc")
        add(15, "V")
        dx(2, 0, 1)
        dw(2, 0, 1, "acc")
        dx(2, 3, 1)
        dx_drain(2, 0, "S")
        dw(2, 0, 2, "acc")
        quant_t(14)
        dx(2, 1, 0, "acc")
        dx_drain(2, 3, "S")
        mask(15)
        dw(2, 0, 3, "acc")
        dx(2, 1, 1)
        dw_drain(2, 0, "S")
        dx(2, 2, 0, "acc")
        dw(2, 1, 3, "gp")
        dx_drain(2, 1, "S")
        transposes(3, 1, 0)
        dw_drain(2, 1, "V")
        token_copy(15, "S")
        transposes(3, 1, 1)
        feature_copy(3, 1, 0, "V")
        dw_store(2, 0)
        dx(2, 2, 1)
        feature_copy(3, 1, 1, "V")
        dx(2, 4, 0, "acc")
        dx_drain(2, 2, "S")
        dx(2, 5, 0, "acc")
        quant_t(15)
        dx(2, 4, 1)
        dx_store(2, 0)
        quant_f(3, 1)
        dx(2, 5, 1)
        dx_drain(2, 4, "S")
        dw(3, 0, 3, "gp")
        dw(3, 1, 3, "acc")
        dw_drain(3, 0, "S")
        dx_drain(2, 5, "V")
        dw(3, 2, 0, "acc")
        dw(3, 3, 0, "gp")
        dw(3, 2, 1, "acc")
        dw_drain(3, 1, "S")
        dw(3, 3, 1, "gp")
        dw(3, 2, 2, "acc")
        dw_store(3, 0)
        dw(3, 3, 2, "gp")
        dw(3, 2, 3, "acc")
        dw(3, 3, 3, "gp")
        dw_drain(3, 2, "S")
        dx(2, 6, 0, "acc")
        dw_drain(3, 3, "V")
        dx(2, 7, 0, "acc")
        dx(2, 6, 1)
        dw_store(3, 1)
        dx(2, 7, 1)
        dx_drain(2, 6, "V")
        dw(2, 2, 0, "tr")
        dx_drain(2, 7, "S")
        dw(2, 3, 0, "gp")
        dw(2, 2, 1, "tr")
        dx_store(2, 1)
        dw(2, 3, 1, "gp")
        dw(2, 2, 2, "tr")
        dw(2, 3, 2, "gp")
        dw(2, 2, 3, "tr")
        dw(2, 3, 3, "gp")
        dw_drain(2, 2, "V")
        dx(3, 0, 0, "acc")
        dw_drain(2, 3, "S")
        dx(3, 1, 0, "acc")
        dx(3, 0, 1)
        dw_store(2, 1)
        dx(3, 1, 1)
        dx_drain(3, 0, "S")
        dx(3, 2, 0, "acc")
        dx(3, 3, 0, "gp")
        dx_drain(3, 1, "V")
        dx(3, 2, 1)
        dx(3, 3, 1)
        dx_drain(3, 2, "V")
        dx(3, 4, 0, "gp")
        dx_store_row(3, 0)
        dx_drain(3, 3, "S")
        dx(3, 5, 0, "tr")
        dx(3, 4, 1)
        dx_store_row(3, 1)
        dx(3, 5, 1)
        dx_drain(3, 4, "V")
        dx(3, 6, 0, "gp")
        dx(3, 6, 1)
        dx_drain(3, 5, "S")
        dx(3, 7, 0, "gp")
        dx_drain(3, 6, "V")
        dx_store_row(3, 2)
        dx(3, 7, 1)
        dx_drain(3, 7, "V")
        dx_store_row(3, 3)
